import numpy as np
import ml_dtypes


def mxq(x, axis, fmt="e4m3"):
    dtype, down = {"e4m3": (ml_dtypes.float8_e4m3fn, 7), "e5m2": (ml_dtypes.float8_e5m2, 14)}[fmt]
    v = np.moveaxis(np.asarray(x, np.float32).astype(ml_dtypes.bfloat16).astype(np.float64), axis, -1)
    blocks = v.reshape(v.shape[:-1] + (-1, 32))
    amax = np.abs(blocks).max(-1, keepdims=True)
    byte = np.maximum(np.where(amax > 0, np.frexp(amax)[1] - 1 + 127, 0) - down, 1)
    scale = np.exp2(byte - 127.0)
    codes = (blocks / scale).astype(np.float32).astype(dtype).astype(np.float64)
    return np.moveaxis((codes * scale).reshape(v.shape), -1, axis)


WIDE = False


def mx_kscale(k):
    if not WIDE:
        return np.ones(k)
    levels = np.array([18, -18])
    if k % 512:
        return np.exp2(np.random.permutation(np.resize(levels, k // 32))).repeat(32)
    a = np.empty((k // 512, 16))
    for p in range(k // 512):
        a[p, :8] = np.random.permutation(np.resize(levels, 8))
        for g in range(8):
            far = levels[np.abs(levels - a[p, g]) >= 10]
            a[p, g + 8] = far[np.random.randint(len(far))]
    return np.exp2(a.ravel()).repeat(32)


BF16 = ml_dtypes.bfloat16


def bf(x):
    return np.asarray(x, np.float32).astype(BF16)


def f64(x):
    return np.asarray(x).astype(np.float64)


B, S, D, H, DK = 2, 512, 768, 8, 128
E = H * DK
T = B * S
EPS = 1e-5


def heads(y):
    return y.reshape(B, S, H, DK).transpose(0, 2, 1, 3)


def merge(g):
    return g.transpose(0, 2, 1, 3).reshape(T, E)


def draw_grad(s, u):
    g = np.random.standard_normal((B, S, E)) * np.exp2(np.random.randint(-6, 1, (B, S, 1))) * 0.5
    return bf(heads(g / s * u))


def setup_inputs():
    s = mx_kscale(T).reshape(B, S, 1)
    u = mx_kscale(3 * E)
    uq, uk, uv = u[:E], u[E:2 * E], u[2 * E:]
    quiet = np.where(np.random.random((B, S, 1)) < 0.1, 0.02, 1.0)
    x0 = bf(np.random.standard_normal((B, S, D)) * quiet)
    g1 = bf(1.0 + 0.1 * np.random.standard_normal(D))
    wq0 = bf(np.random.standard_normal((E, D)) / np.sqrt(D))
    wk0 = bf(np.random.standard_normal((E, D)) / np.sqrt(D))
    wv0 = bf(np.random.standard_normal((E, D)) * 2.0 / np.sqrt(D))
    xf = f64(x0)
    r = 1.0 / np.sqrt(np.sum(xf * xf, axis=-1) / D + EPS)
    grad_0 = draw_grad(s, uq)
    grad_1 = draw_grad(s, uk)
    grad_2 = draw_grad(s, uv)
    return {"x": bf(f64(x0) * s),
            "g1": g1,
            "wq": bf(f64(wq0) / uq[:, None]),
            "wk": bf(f64(wk0) / uk[:, None]),
            "wv": bf(f64(wv0) / uv[:, None]),
            "r": np.asarray(r, np.float32),
            "grad_0": grad_0, "grad_1": grad_1, "grad_2": grad_2}


def reference(x, g1, wq, wk, wv, r, grad_0, grad_1, grad_2):
    xf = f64(x).reshape(T, D)
    rf = f64(r).reshape(T, 1)
    gain = f64(g1)
    xn = xf * rf * gain
    dy = np.concatenate([merge(f64(grad_0)), merge(f64(grad_1)), merge(f64(grad_2))], axis=1)
    w = np.concatenate([f64(wq), f64(wk), f64(wv)], axis=0)
    dxn = mxq(dy, 1, "e5m2") @ mxq(w, 0, "e4m3")
    dw = mxq(dy, 0, "e5m2").T @ mxq(xn, 0, "e4m3")
    h = dxn * gain
    m = np.sum(h * xf, axis=1, keepdims=True) / D
    dx = rf * h - rf * rf * rf * xf * m
    return dx.reshape(B, S, D), dw[:E], dw[E:2 * E], dw[2 * E:]

@@ -1,0 +1,468 @@
+from contextlib import ExitStack
+
+import concourse.mybir as mybir
+from concourse.masks import make_identity
+
+F32 = mybir.dt.float32
+BF16 = mybir.dt.bfloat16
+U32 = mybir.dt.uint32
+U8 = mybir.dt.uint8
+E4 = mybir.dt.float8_e4m3fn_x4
+E5 = mybir.dt.float8_e5m2_x4
+MULT = mybir.AluOpType.mult
+ADD = mybir.AluOpType.add
+COPY = mybir.ActivationFunctionType.Copy
+
+B, S, D, H, DK = 2, 512, 768, 8, 128
+E = H * DK
+T = B * S
+P = 128
+J = 4
+FLOPS = 2 * 2 * T * 3 * E * D
+
+
+def tile_transformerblock_pa_v_kernel(
+    tc, x, g1, wq, wk, wv, r, grad_0, grad_1, grad_2, out_0, out_1, out_2, out_3
+):
+    nc = tc.nc
+    grads = (grad_0, grad_1, grad_2)
+    weights = (wq, wk, wv)
+    w_outs = (out_1, out_2, out_3)
+
+    with ExitStack() as ctx:
+        keep = ctx.enter_context(tc.tile_pool(name="keep", bufs=1))
+        rot = ctx.enter_context(tc.tile_pool(name="rot", bufs=2))
+        ps_tr = ctx.enter_context(tc.psum_pool(name="ps_tr", bufs=3))
+        ps_mm = ctx.enter_context(tc.psum_pool(name="ps_mm", bufs=5))
+        ctx.enter_context(tc.manual_schedule())
+
+        ident = keep.tile([P, P], F32, name="ident")
+        ones = keep.tile([P, P], BF16, name="ones")
+        g_row = keep.tile([P, D], BF16, name="g_row")
+        g_bc = keep.tile([P, D], F32, name="g_bc")
+        g_col = keep.tile([P, 2], F32, name="g_col")
+        r_sb = keep.tile([P, B, J], F32, name="r_sb")
+        nr2 = keep.tile([P, B, J], F32, name="nr2")
+        c_sb = keep.tile([P, B, J], F32, name="c_sb")
+        x_sb = keep.tile([P, B, J, D], BF16, name="x_sb")
+        dummy = keep.tile([P, 1], F32, name="dummy")
+        dyf_c = keep.tile([P, 6, T], U32, name="dyf_c", align_bytes=64)
+        dyf_s = keep.tile([P, 6, T], U8, name="dyf_s", align_bytes=64)
+        w_c = keep.tile([P, 6, D], U32, name="w_c", align_bytes=64)
+        w_s = keep.tile([P, 6, D], U8, name="w_s", align_bytes=64)
+        xn_c = keep.tile([P, B, D], U32, name="xn_c", align_bytes=64)
+        xn_s = keep.tile([P, B, D], U8, name="xn_s", align_bytes=64)
+
+        raw = {}
+        dyt = {}
+        big = {}
+        gf = {}
+        gt = {}
+        gw = {}
+        gx = {}
+        bank = {}
+        hT = {}
+        res = {}
+
+        def load_x(b):
+            nc.sync.dma_start(out=x_sb[:, b], in_=x[b].rearrange("(p j) d -> p j d", j=J))
+
+        def load_dy(a, b):
+            t = rot.tile([P, J, E], BF16, name="dy_raw", bufs=4)
+            raw[a, b] = t
+            src = grads[a][b].rearrange("h (p j) d -> p j h d", j=J)
+            for j in range(J):
+                nc.sync.dma_start(
+                    out=t[:, j, :].rearrange("p (h d) -> p h d", d=DK), in_=src[:, j]
+                )
+
+        def load_w(g):
+            t = rot.tile([P, J, D], BF16, name="w_raw", bufs=3)
+            raw["w", g] = t
+            a, half = divmod(g, 2)
+            src = weights[a][512 * half : 512 * half + 512, :]
+            nc.sync.dma_start(out=t[:], in_=src.rearrange("(p j) d -> p j d", j=J))
+
+        def xr(b):
+            t = rot.tile([P, J, D], F32, name="big", bufs=2)
+            big[b] = t
+            for j in range(J):
+                nc.scalar.activation(
+                    out=t[:, j, :], in_=x_sb[:, b, j, :], func=COPY, scale=r_sb[:, b, j : j + 1]
+                )
+
+        def xn(b):
+            t = rot.tile([P, D, J], BF16, name="gw", bufs=2, align_bytes=64)
+            gx[b] = t
+            nc.vector.tensor_tensor(
+                out=t[:],
+                in0=big[b][:].rearrange("p j d -> p d j"),
+                in1=g_bc[:].unsqueeze(2).to_broadcast([P, D, J]),
+                op=MULT,
+            )
+
+        def quant_d(codes, scales, src, fmt):
+            flat = src[:].rearrange("p d j -> p (d j)")
+            for lo, hi in ((0, 512), (512, 768)):
+                nc.vector.quantize_mx(
+                    out=codes[:, lo:hi].bitcast(fmt), scales=scales[:, lo:hi], in_=flat[:, 4 * lo : 4 * hi]
+                )
+
+        def xq(b):
+            quant_d(xn_c[:, b, :], xn_s[:, b, :], gx[b], E4)
+
+        def tr(a, b, g):
+            words = raw[a, b][:].rearrange("p j f -> p (j f)").bitcast(F32)
+            for jj in range(2):
+                t = ps_tr.tile([P, 2, 2, P], F32, name="tr")
+                bank[a, b, g, jj] = t
+                for j2 in range(2):
+                    for u in range(2):
+                        lo = (2 * jj + j2) * (E // 2) + 256 * g
+                        nc.tensor.transpose(t[:, j2, u, :], words[:, lo + u : lo + 256 : 2], ident[:])
+
+        def fe(a, b, g):
+            t = rot.tile([P, 2048], BF16, name="gf", bufs=3, align_bytes=64)
+            gf[a, b, g] = t
+            words = t[:].bitcast(F32)
+            for jj in range(2):
+                nc.scalar.copy(
+                    out=words[:, 512 * jj : 512 * jj + 512].rearrange("p (j q u) -> p j q u", j=2, u=2),
+                    in_=bank[a, b, g, jj][:].rearrange("p j u q -> p j q u"),
+                )
+
+        def qf(a, b, g):
+            n = 2 * a + g
+            nc.vector.quantize_mx(
+                out=dyf_c[:, n, S * b : S * b + S].bitcast(E5),
+                scales=dyf_s[:, n, S * b : S * b + S],
+                in_=gf[a, b, g][:],
+            )
+
+        def interleave(eng, out, in_):
+            o = out.rearrange("p (c i) j -> p c j i", i=4)
+            n = in_.rearrange("p j (c i) -> p c j i", i=4)
+            if eng is nc.scalar:
+                nc.scalar.copy(out=o, in_=n)
+            else:
+                nc.vector.tensor_copy(out=o, in_=n)
+
+        def it(a, b, g, eng, pieces=1):
+            t = rot.tile([P, 512, J], BF16, name="gt", bufs=3, align_bytes=64)
+            gt[a, b, g] = t
+            n = 512 // pieces
+            for k in range(pieces):
+                lo = n * k
+                interleave(eng, t[:, lo : lo + n, :], raw[a, b][:, :, 512 * g + lo : 512 * g + lo + n])
+
+        def qt(a, b, g):
+            if a not in dyt:
+                dyt[a] = (
+                    rot.tile([P, B, E], U32, name="dyt_c", align_bytes=64),
+                    rot.tile([P, B, E], U8, name="dyt_s", align_bytes=64),
+                )
+            codes, scales = dyt[a]
+            nc.vector.quantize_mx(
+                out=codes[:, b, 512 * g : 512 * g + 512].bitcast(E5),
+                scales=scales[:, b, 512 * g : 512 * g + 512],
+                in_=gt[a, b, g][:].rearrange("p f j -> p (f j)"),
+            )
+
+        def iw(g, eng=None):
+            t = rot.tile([P, D, J], BF16, name="gw", bufs=2, align_bytes=64)
+            gw[g] = t
+            interleave(nc.vector, t[:], raw["w", g][:])
+
+        def qw(g):
+            quant_d(w_c[:, g, :], w_s[:, g, :], gw[g], E4)
+
+        def dw_mm(a, h):
+            codes, scales = dyt[a]
+            p0 = ps_mm.tile([P, 512], F32, name="mm")
+            p1 = ps_mm.tile([P, 512], F32, name="mm")
+            bank["dw", a, h] = (p0, p1)
+            for b in range(B):
+                for pt, lo in ((p0, 0), (p1, 256)):
+                    nc.tensor.matmul_mx(
+                        out=pt[:],
+                        lhsT=codes[:, b, P * h : P * h + P].bitcast(E5),
+                        lhsT_scale=scales[:, b, P * h : P * h + P],
+                        rhs=xn_c[:, b, lo : lo + 512].bitcast(E4),
+                        rhs_scale=xn_s[:, b, lo : lo + 512],
+                        start=(b == 0),
+                        stop=(b == B - 1),
+                    )
+
+        def dw_ev(a, h, eng=None):
+            p0, p1 = bank["dw", a, h]
+            t = rot.tile([P, D], F32, name="res", bufs=4)
+            res[a, h] = t
+            if eng is nc.vector:
+                nc.vector.tensor_copy(out=t[:, 0:512], in_=p0[:])
+                nc.vector.tensor_copy(out=t[:, 512:768], in_=p1[:, 256:512])
+            else:
+                nc.scalar.copy(out=t[:, 0:512], in_=p0[:])
+                nc.scalar.copy(out=t[:, 512:768], in_=p1[:, 256:512])
+
+        def dw_st(a, h, eng):
+            eng.dma_start(out=w_outs[a][P * h : P * h + P, :], in_=res[a, h][:])
+
+        def dxt_mm(b):
+            for i in range(2):
+                pt = ps_mm.tile([P, 512], F32, name="mm")
+                bank["dxt", b, i] = pt
+                d0 = 512 + P * i
+                for n in range(6):
+                    nc.tensor.matmul_mx(
+                        out=pt[:],
+                        lhsT=w_c[:, n, d0 : d0 + P].bitcast(E4),
+                        lhsT_scale=w_s[:, n, d0 : d0 + P],
+                        rhs=dyf_c[:, n, S * b : S * b + S].bitcast(E5),
+                        rhs_scale=dyf_s[:, n, S * b : S * b + S],
+                        start=(n == 0),
+                        stop=(n == 5),
+                    )
+
+        def dxt_ev(b):
+            t = rot.tile([P, 2, 512], F32, name="hT", bufs=1)
+            hT[b] = t
+            for i in range(2):
+                nc.scalar.activation(
+                    out=t[:, i, :], in_=bank["dxt", b, i][:], func=COPY, scale=g_col[:, i : i + 1]
+                )
+
+        def dxt_tr(b):
+            for jj in range(2):
+                t = ps_tr.tile([P, 2, 2, P], F32, name="tr")
+                bank["dxr", b, jj] = t
+                for j2 in range(2):
+                    for i in range(2):
+                        j = 2 * jj + j2
+                        nc.tensor.transpose(t[:, j2, i, :], hT[b][:, i, P * j : P * j + P], ident[:])
+
+        def dxt_sc(b, j):
+            if ("h", b) not in big:
+                big["h", b] = rot.tile([P, J, D], F32, name="big", bufs=2)
+            nc.scalar.activation(
+                out=big["h", b][:, j, 512:768],
+                in_=bank["dxr", b, j // 2][:, j % 2].rearrange("p i q -> p (i q)"),
+                func=COPY,
+                scale=r_sb[:, b, j : j + 1],
+            )
+
+        def dxm_mm(b, j):
+            pt = ps_mm.tile([P, 512], F32, name="mm")
+            bank["dxm", b, j] = pt
+            t0 = S * b + P * j
+            for n in range(6):
+                nc.tensor.matmul_mx(
+                    out=pt[:],
+                    lhsT=dyf_c[:, n, t0 : t0 + P].bitcast(E5),
+                    lhsT_scale=dyf_s[:, n, t0 : t0 + P],
+                    rhs=w_c[:, n, 0:512].bitcast(E4),
+                    rhs_scale=w_s[:, n, 0:512],
+                    start=(n == 0),
+                    stop=(n == 5),
+                )
+
+        def dx1(b, j):
+            if ("h", b) not in big:
+                big["h", b] = rot.tile([P, J, D], F32, name="big", bufs=2)
+            nc.vector.scalar_tensor_tensor(
+                out=big["h", b][:, j, 0:512],
+                in0=bank["dxm", b, j][:],
+                scalar=r_sb[:, b, j : j + 1],
+                in1=g_bc[:, 0:512],
+                op0=MULT,
+                op1=MULT,
+            )
+
+        def dx2(b, j):
+            junk = rot.tile([P, D], F32, name="junk", bufs=1)
+            nc.vector.scalar_tensor_tensor(
+                out=junk[:],
+                in0=big["h", b][:, j, :],
+                scalar=nr2[:, b, j : j + 1],
+                in1=x_sb[:, b, j, :],
+                op0=MULT,
+                op1=MULT,
+                accum_out=c_sb[:, b, j : j + 1],
+            )
+
+        def dx3(b, j):
+            nc.vector.scalar_tensor_tensor(
+                out=big["h", b][:, j, :],
+                in0=x_sb[:, b, j, :],
+                scalar=c_sb[:, b, j : j + 1],
+                in1=big["h", b][:, j, :],
+                op0=MULT,
+                op1=ADD,
+            )
+
+        def dx_st(b, j):
+            dst = out_0[b].rearrange("(p j) d -> p j d", j=J)
+            nc.sync.dma_start(out=dst[:, j], in_=big["h", b][:, j, :])
+
+        nc.gpsimd.memset(g_row[:], 0.0)
+        nc.gpsimd.memset(ones[:], 1.0)
+        make_identity(nc, ident[:])
+        nc.sync.dma_start(out=g_row[0:1, :], in_=g1.rearrange("(o d) -> o d", o=1))
+        nc.sync.dma_start(out=r_sb[:], in_=r.rearrange("b (p j) -> p b j", j=J))
+        load_x(0)
+        load_dy(0, 0)
+        load_x(1)
+        load_dy(0, 1)
+        load_dy(1, 0)
+        load_dy(1, 1)
+        load_w(0)
+        load_w(1)
+        load_w(2)
+        nc.vector.memset(dummy[:], 0.0)
+        nc.scalar.activation(out=dummy[:], in_=dummy[:], func=COPY)
+
+        gp0 = ps_mm.tile([P, 512], F32, name="mm")
+        gp1 = ps_mm.tile([P, 512], F32, name="mm")
+        nc.tensor.matmul(gp0[:], lhsT=ones[:], rhs=g_row[:, 0:512], start=True, stop=True)
+        nc.tensor.matmul(gp1[:, 0:256], lhsT=ones[:], rhs=g_row[:, 512:768], start=True, stop=True)
+        nc.scalar.copy(out=g_bc[:, 0:512], in_=gp0[:])
+        nc.scalar.copy(out=g_bc[:, 512:768], in_=gp1[:, 0:256])
+        gp2 = ps_tr.tile([P, 2, 2, P], F32, name="tr")
+        for i in range(2):
+            nc.tensor.transpose(gp2[:, 0, i, :], g_bc[:, 512 + P * i : 640 + P * i], ident[:])
+        nc.vector.tensor_copy(out=g_col[:], in_=gp2[:, 0, :, 0])
+        nc.vector.scalar_tensor_tensor(
+            out=nr2[:], in0=r_sb[:], scalar=-1.0 / D, in1=r_sb[:], op0=MULT, op1=MULT
+        )
+
+        xr(0)
+        tr(0, 0, 0)
+        fe(0, 0, 0)
+        xn(0)
+        xr(1)
+        it(0, 0, 0, nc.vector)
+        xq(0)
+        tr(0, 0, 1)
+        fe(0, 0, 1)
+        xn(1)
+        qt(0, 0, 0)
+        it(0, 1, 0, nc.vector)
+        xq(1)
+        qf(0, 0, 0)
+        qt(0, 1, 0)
+        tr(0, 1, 0)
+        fe(0, 1, 0)
+        it(0, 0, 1, nc.vector)
+        qf(0, 0, 1)
+        it(0, 1, 1, nc.vector)
+        qt(0, 0, 1)
+        tr(0, 1, 1)
+        fe(0, 1, 1)
+        qf(0, 1, 0)
+        qt(0, 1, 1)
+        load_dy(2, 0)
+        load_dy(2, 1)
+
+        halves = [(a, b, g) for a in (1, 2) for b in range(B) for g in range(2)]
+        w_iw = {1: 0, 3: 1, 4: 2, 5: 3, 6: 4, 7: 5}
+        prev = (0, 1, 1)
+        pend = None
+        for i, (a, b, g) in enumerate(halves):
+            tr(a, b, g)
+            fe(a, b, g)
+            if a == 1:
+                it(a, b, g, nc.vector)
+            if pend is not None:
+                qw(pend)
+                if pend + 3 < 6:
+                    load_w(pend + 3)
+                pend = None
+            qf(*prev)
+            prev = (a, b, g)
+            if i in w_iw:
+                iw(w_iw[i])
+                pend = w_iw[i]
+            if a == 1:
+                qt(a, b, g)
+            for h in (2 * (i % 4), 2 * (i % 4) + 1):
+                dw_mm(a - 1, h)
+                dw_ev(a - 1, h)
+                dw_st(a - 1, h, nc.scalar if a == 1 else nc.sync)
+        qf(*prev)
+        qw(pend)
+
+        dxt_mm(0)
+        dxt_ev(0)
+        it(2, 0, 0, nc.scalar, 2)
+        dxm_mm(0, 0)
+        dx1(0, 0)
+        dxm_mm(0, 1)
+        dx1(0, 1)
+        dxt_tr(0)
+        dxt_sc(0, 0)
+        dxt_sc(0, 1)
+        dxt_sc(0, 2)
+        dxt_sc(0, 3)
+        it(2, 1, 0, nc.scalar, 2)
+        qt(2, 0, 0)
+        dx2(0, 0)
+        dx2(0, 1)
+        dx3(0, 0)
+        dx_st(0, 0)
+        dx3(0, 1)
+        dx_st(0, 1)
+        qt(2, 1, 0)
+        dxm_mm(0, 2)
+        dx1(0, 2)
+        dxm_mm(0, 3)
+        dx1(0, 3)
+        it(2, 0, 1, nc.scalar, 2)
+        dx2(0, 2)
+        dx2(0, 3)
+        dx3(0, 2)
+        dx_st(0, 2)
+        dx3(0, 3)
+        dx_st(0, 3)
+        for h in (0, 1):
+            dw_mm(2, h)
+            dw_ev(2, h)
+            dw_st(2, h, nc.sync)
+        it(2, 1, 1, nc.scalar, 2)
+        qt(2, 0, 1)
+        dxt_mm(1)
+        dxt_ev(1)
+        dxm_mm(1, 0)
+        dx1(1, 0)
+        dxm_mm(1, 1)
+        dx1(1, 1)
+        qt(2, 1, 1)
+        dxt_tr(1)
+        for j in range(J):
+            dxt_sc(1, j)
+        dx2(1, 0)
+        dx2(1, 1)
+        dx3(1, 0)
+        dx_st(1, 0)
+        dx3(1, 1)
+        dx_st(1, 1)
+        for h in (2, 3):
+            dw_mm(2, h)
+            dw_ev(2, h)
+            dw_st(2, h, nc.sync)
+        dxm_mm(1, 2)
+        dx1(1, 2)
+        dxm_mm(1, 3)
+        dx1(1, 3)
+        for h in (4, 5):
+            dw_mm(2, h)
+            dw_ev(2, h)
+            dw_st(2, h, nc.sync)
+        dx2(1, 2)
+        dx2(1, 3)
+        dx3(1, 2)
+        dx_st(1, 2)
+        dx3(1, 3)
+        dx_st(1, 3)
+        for h in (6, 7):
+            dw_mm(2, h)
+            dw_ev(2, h)
+            dw_st(2, h, nc.sync)

@@ -18,6 +18,7 @@ E = H * DK
 T = B * S
 P = 128
 J = 4
+PRE = (1, 2)
 FLOPS = 2 * 2 * T * 3 * E * D
 
 
@@ -25,6 +26,7 @@ def tile_transformerblock_pa_v_kernel(
     tc, x, g1, wq, wk, wv, r, grad_0, grad_1, grad_2, out_0, out_1, out_2, out_3
 ):
     nc = tc.nc
+    V, A = nc.vector, nc.scalar
     grads = (grad_0, grad_1, grad_2)
     weights = (wq, wk, wv)
     w_outs = (out_1, out_2, out_3)
@@ -32,8 +34,9 @@ def tile_transformerblock_pa_v_kernel(
     with ExitStack() as ctx:
         keep = ctx.enter_context(tc.tile_pool(name="keep", bufs=1))
         rot = ctx.enter_context(tc.tile_pool(name="rot", bufs=2))
-        ps_tr = ctx.enter_context(tc.psum_pool(name="ps_tr", bufs=3))
-        ps_mm = ctx.enter_context(tc.psum_pool(name="ps_mm", bufs=5))
+        ps_tr = ctx.enter_context(tc.psum_pool(name="ps_tr", bufs=2))
+        ps_mm = ctx.enter_context(tc.psum_pool(name="ps_mm", bufs=4))
+        ps_dx = ctx.enter_context(tc.psum_pool(name="ps_dx", bufs=2))
         ctx.enter_context(tc.manual_schedule())
 
         ident = keep.tile([P, P], F32, name="ident")
@@ -45,7 +48,6 @@ def tile_transformerblock_pa_v_kernel(
         nr2 = keep.tile([P, B, J], F32, name="nr2")
         c_sb = keep.tile([P, B, J], F32, name="c_sb")
         x_sb = keep.tile([P, B, J, D], BF16, name="x_sb")
-        dummy = keep.tile([P, 1], F32, name="dummy")
         dyf_c = keep.tile([P, 6, T], U32, name="dyf_c", align_bytes=64)
         dyf_s = keep.tile([P, 6, T], U8, name="dyf_s", align_bytes=64)
         w_c = keep.tile([P, 6, D], U32, name="w_c", align_bytes=64)
@@ -53,82 +55,104 @@ def tile_transformerblock_pa_v_kernel(
         xn_c = keep.tile([P, B, D], U32, name="xn_c", align_bytes=64)
         xn_s = keep.tile([P, B, D], U8, name="xn_s", align_bytes=64)
 
-        raw = {}
-        dyt = {}
-        big = {}
-        gf = {}
-        gt = {}
-        gw = {}
-        gx = {}
-        bank = {}
-        hT = {}
-        res = {}
+        tiles = {}
+
+        def get(pool, shape, dtype, tag, key, bufs, align=None):
+            if (tag, key) not in tiles:
+                if align:
+                    t = pool.tile(shape, dtype, name=tag, bufs=bufs, align_bytes=align)
+                else:
+                    t = pool.tile(shape, dtype, name=tag, bufs=bufs)
+                tiles[tag, key] = t
+            return tiles[tag, key]
 
         def load_x(b):
-            nc.sync.dma_start(out=x_sb[:, b], in_=x[b].rearrange("(p j) d -> p j d", j=J))
+            src = x[b].rearrange("(p j) d -> p j d", j=J)
+            step = 256 if b == 0 else D
+            for lo in range(0, D, step):
+                nc.sync.dma_start(out=x_sb[:, b, :, lo : lo + step], in_=src[:, :, lo : lo + step])
+
+        def dy_raw(a, b):
+            return get(rot, [P, J, E], BF16, "dy_raw", (a, b), 4)
 
         def load_dy(a, b):
-            t = rot.tile([P, J, E], BF16, name="dy_raw", bufs=4)
-            raw[a, b] = t
+            if a in PRE:
+                src = grads[a][b].rearrange("h (p j) d -> p h (j d)", j=J)
+                flat = dy_raw(a, b)[:].rearrange("p j f -> p (j f)").rearrange("p (h k) -> p h k", h=H)
+                for g in range(2):
+                    nc.sync.dma_start(out=flat[:, 4 * g : 4 * g + 4], in_=src[:, 4 * g : 4 * g + 4])
+                return
             src = grads[a][b].rearrange("h (p j) d -> p j h d", j=J)
             for j in range(J):
                 nc.sync.dma_start(
-                    out=t[:, j, :].rearrange("p (h d) -> p h d", d=DK), in_=src[:, j]
+                    out=dy_raw(a, b)[:, j, :].rearrange("p (h d) -> p h d", d=DK), in_=src[:, j]
                 )
 
-        def load_w(g):
-            t = rot.tile([P, J, D], BF16, name="w_raw", bufs=3)
-            raw["w", g] = t
-            a, half = divmod(g, 2)
-            src = weights[a][512 * half : 512 * half + 512, :]
-            nc.sync.dma_start(out=t[:], in_=src.rearrange("(p j) d -> p j d", j=J))
+        def ps(a, b, g, eng):
+            t = get(rot, [P, J, 2, P], F32, "srt", (a, b, g), 2)
+            words = dy_raw(a, b)[:].rearrange("p j f -> p (j f)").bitcast(F32)
+            words = words.rearrange("p (h j w) -> p h j w", h=H, j=J)
+            for u in range(2):
+                o = t[:, :, u, :].rearrange("p j (h q) -> p j h q", h=4)
+                n = words[:, 4 * g : 4 * g + 4, :, u::2].rearrange("p h j q -> p j h q")
+                if eng is A:
+                    nc.scalar.copy(out=o, in_=n)
+                else:
+                    nc.vector.tensor_copy(out=o, in_=n)
 
-        def xr(b):
-            t = rot.tile([P, J, D], F32, name="big", bufs=2)
-            big[b] = t
+        def w_raw(n):
+            return get(rot, [P, J, D], BF16, "w_raw", n, 3)
+
+        def load_w(n):
+            a, half = divmod(n, 2)
+            src = weights[a][512 * half : 512 * half + 512, :]
+            nc.sync.dma_start(out=w_raw(n)[:], in_=src.rearrange("(p j) d -> p j d", j=J))
+
+        def grouped_d(key):
+            return get(rot, [P, D, J], BF16, "gw", key, 2, 64)
+
+        def norm(b, k):
+            lo, hi = 256 * k, 256 * k + 256
+            t = get(rot, [P, J, D], F32, "big", ("x", b), 2)
             for j in range(J):
                 nc.scalar.activation(
-                    out=t[:, j, :], in_=x_sb[:, b, j, :], func=COPY, scale=r_sb[:, b, j : j + 1]
+                    out=t[:, j, lo:hi], in_=x_sb[:, b, j, lo:hi], func=COPY, scale=r_sb[:, b, j : j + 1]
                 )
-
-        def xn(b):
-            t = rot.tile([P, D, J], BF16, name="gw", bufs=2, align_bytes=64)
-            gx[b] = t
             nc.vector.tensor_tensor(
-                out=t[:],
-                in0=big[b][:].rearrange("p j d -> p d j"),
-                in1=g_bc[:].unsqueeze(2).to_broadcast([P, D, J]),
+                out=grouped_d(("x", b))[:, lo:hi, :],
+                in0=t[:, :, lo:hi].rearrange("p j d -> p d j"),
+                in1=g_bc[:, lo:hi].unsqueeze(2).to_broadcast([P, hi - lo, J]),
                 op=MULT,
             )
 
-        def quant_d(codes, scales, src, fmt):
+        def quant_d(codes, scales, src):
             flat = src[:].rearrange("p d j -> p (d j)")
             for lo, hi in ((0, 512), (512, 768)):
                 nc.vector.quantize_mx(
-                    out=codes[:, lo:hi].bitcast(fmt), scales=scales[:, lo:hi], in_=flat[:, 4 * lo : 4 * hi]
+                    out=codes[:, lo:hi].bitcast(E4), scales=scales[:, lo:hi], in_=flat[:, 4 * lo : 4 * hi]
                 )
 
         def xq(b):
-            quant_d(xn_c[:, b, :], xn_s[:, b, :], gx[b], E4)
+            quant_d(xn_c[:, b, :], xn_s[:, b, :], grouped_d(("x", b)))
 
-        def tr(a, b, g):
-            words = raw[a, b][:].rearrange("p j f -> p (j f)").bitcast(F32)
+        def feat(a, b, g):
+            words = dy_raw(a, b)[:].rearrange("p j f -> p (j f)").bitcast(F32)
+            t = get(rot, [P, 2048], BF16, "gf", (a, b, g), 3, 64)
+            out_words = t[:].bitcast(F32)
             for jj in range(2):
-                t = ps_tr.tile([P, 2, 2, P], F32, name="tr")
-                bank[a, b, g, jj] = t
+                ps = ps_tr.tile([P, 2, 2, P], F32, name="tr")
                 for j2 in range(2):
                     for u in range(2):
-                        lo = (2 * jj + j2) * (E // 2) + 256 * g
-                        nc.tensor.transpose(t[:, j2, u, :], words[:, lo + u : lo + 256 : 2], ident[:])
-
-        def fe(a, b, g):
-            t = rot.tile([P, 2048], BF16, name="gf", bufs=3, align_bytes=64)
-            gf[a, b, g] = t
-            words = t[:].bitcast(F32)
-            for jj in range(2):
+                        j = 2 * jj + j2
+                        lo = j * (E // 2) + 256 * g
+                        if a in PRE:
+                            src = tiles["srt", (a, b, g)][:, j, u, :]
+                        else:
+                            src = words[:, lo + u : lo + 256 : 2]
+                        nc.tensor.transpose(ps[:, j2, u, :], src, ident[:])
                 nc.scalar.copy(
-                    out=words[:, 512 * jj : 512 * jj + 512].rearrange("p (j q u) -> p j q u", j=2, u=2),
-                    in_=bank[a, b, g, jj][:].rearrange("p j u q -> p j q u"),
+                    out=out_words[:, 512 * jj : 512 * jj + 512].rearrange("p (j q u) -> p j q u", j=2, u=2),
+                    in_=ps[:].rearrange("p j u q -> p j q u"),
                 )
 
         def qf(a, b, g):
@@ -136,51 +160,57 @@ def tile_transformerblock_pa_v_kernel(
             nc.vector.quantize_mx(
                 out=dyf_c[:, n, S * b : S * b + S].bitcast(E5),
                 scales=dyf_s[:, n, S * b : S * b + S],
-                in_=gf[a, b, g][:],
+                in_=tiles["gf", (a, b, g)][:],
             )
 
         def interleave(eng, out, in_):
             o = out.rearrange("p (c i) j -> p c j i", i=4)
             n = in_.rearrange("p j (c i) -> p c j i", i=4)
-            if eng is nc.scalar:
+            if eng is A:
                 nc.scalar.copy(out=o, in_=n)
             else:
                 nc.vector.tensor_copy(out=o, in_=n)
 
-        def it(a, b, g, eng, pieces=1):
-            t = rot.tile([P, 512, J], BF16, name="gt", bufs=3, align_bytes=64)
-            gt[a, b, g] = t
-            n = 512 // pieces
-            for k in range(pieces):
-                lo = n * k
-                interleave(eng, t[:, lo : lo + n, :], raw[a, b][:, :, 512 * g + lo : 512 * g + lo + n])
+        def it(a, b, g, k, eng):
+            t = get(rot, [P, 512, J], BF16, "gt", (a, b, g), 3, 64)
+            lo = 256 * k
+            if a in PRE:
+                flat = dy_raw(a, b)[:].rearrange("p j f -> p (j f)")
+                raw = flat.rearrange("p (h j d) -> p h j d", h=H, j=J)[:, 4 * g + 2 * k : 4 * g + 2 * k + 2]
+                o = t[:, lo : lo + 256, :].rearrange("p (h c i) j -> p h c j i", h=2, i=4)
+                n = raw.rearrange("p h j (c i) -> p h c j i", i=4)
+                if eng is A:
+                    nc.scalar.copy(out=o, in_=n)
+                else:
+                    nc.vector.tensor_copy(out=o, in_=n)
+                return
+            interleave(eng, t[:, lo : lo + 256, :], dy_raw(a, b)[:, :, 512 * g + lo : 512 * g + lo + 256])
+
+        def dyt(a):
+            return (
+                get(rot, [P, B, E], U32, "dyt_c", a, 2, 64),
+                get(rot, [P, B, E], U8, "dyt_s", a, 2, 64),
+            )
 
         def qt(a, b, g):
-            if a not in dyt:
-                dyt[a] = (
-                    rot.tile([P, B, E], U32, name="dyt_c", align_bytes=64),
-                    rot.tile([P, B, E], U8, name="dyt_s", align_bytes=64),
-                )
-            codes, scales = dyt[a]
+            codes, scales = dyt(a)
             nc.vector.quantize_mx(
                 out=codes[:, b, 512 * g : 512 * g + 512].bitcast(E5),
                 scales=scales[:, b, 512 * g : 512 * g + 512],
-                in_=gt[a, b, g][:].rearrange("p f j -> p (f j)"),
+                in_=tiles["gt", (a, b, g)][:].rearrange("p f j -> p (f j)"),
             )
 
-        def iw(g, eng=None):
-            t = rot.tile([P, D, J], BF16, name="gw", bufs=2, align_bytes=64)
-            gw[g] = t
-            interleave(nc.vector, t[:], raw["w", g][:])
+        def iw(n, k, eng):
+            lo, hi = 256 * k, 256 * k + 256
+            interleave(eng, grouped_d(n)[:, lo:hi, :], w_raw(n)[:, :, lo:hi])
 
-        def qw(g):
-            quant_d(w_c[:, g, :], w_s[:, g, :], gw[g], E4)
+        def qw(n):
+            quant_d(w_c[:, n, :], w_s[:, n, :], grouped_d(n))
 
-        def dw_mm(a, h):
-            codes, scales = dyt[a]
+        def dw(a, h, eng):
+            codes, scales = dyt(a)
             p0 = ps_mm.tile([P, 512], F32, name="mm")
             p1 = ps_mm.tile([P, 512], F32, name="mm")
-            bank["dw", a, h] = (p0, p1)
             for b in range(B):
                 for pt, lo in ((p0, 0), (p1, 256)):
                     nc.tensor.matmul_mx(
@@ -192,69 +222,54 @@ def tile_transformerblock_pa_v_kernel(
                         start=(b == 0),
                         stop=(b == B - 1),
                     )
-
-        def dw_ev(a, h, eng=None):
-            p0, p1 = bank["dw", a, h]
             t = rot.tile([P, D], F32, name="res", bufs=4)
-            res[a, h] = t
-            if eng is nc.vector:
-                nc.vector.tensor_copy(out=t[:, 0:512], in_=p0[:])
-                nc.vector.tensor_copy(out=t[:, 512:768], in_=p1[:, 256:512])
-            else:
-                nc.scalar.copy(out=t[:, 0:512], in_=p0[:])
-                nc.scalar.copy(out=t[:, 512:768], in_=p1[:, 256:512])
+            move = nc.scalar.copy if eng is A else nc.vector.tensor_copy
+            move(out=t[:, 0:512], in_=p0[:])
+            move(out=t[:, 512:768], in_=p1[:, 256:512])
+            nc.sync.dma_start(out=w_outs[a][P * h : P * h + P, :], in_=t[:])
 
-        def dw_st(a, h, eng):
-            eng.dma_start(out=w_outs[a][P * h : P * h + P, :], in_=res[a, h][:])
-
-        def dxt_mm(b):
-            for i in range(2):
-                pt = ps_mm.tile([P, 512], F32, name="mm")
-                bank["dxt", b, i] = pt
-                d0 = 512 + P * i
-                for n in range(6):
-                    nc.tensor.matmul_mx(
-                        out=pt[:],
-                        lhsT=w_c[:, n, d0 : d0 + P].bitcast(E4),
-                        lhsT_scale=w_s[:, n, d0 : d0 + P],
-                        rhs=dyf_c[:, n, S * b : S * b + S].bitcast(E5),
-                        rhs_scale=dyf_s[:, n, S * b : S * b + S],
-                        start=(n == 0),
-                        stop=(n == 5),
-                    )
-
-        def dxt_ev(b):
-            t = rot.tile([P, 2, 512], F32, name="hT", bufs=1)
-            hT[b] = t
-            for i in range(2):
-                nc.scalar.activation(
-                    out=t[:, i, :], in_=bank["dxt", b, i][:], func=COPY, scale=g_col[:, i : i + 1]
+        def dxt(b, i, part):
+            pt = get(ps_dx, [P, 512], F32, "dx", ("t", b, i), 2)
+            d0 = 512 + P * i
+            for n in (range(4), range(4, 6))[part]:
+                nc.tensor.matmul_mx(
+                    out=pt[:],
+                    lhsT=w_c[:, n, d0 : d0 + P].bitcast(E4),
+                    lhsT_scale=w_s[:, n, d0 : d0 + P],
+                    rhs=dyf_c[:, n, S * b : S * b + S].bitcast(E5),
+                    rhs_scale=dyf_s[:, n, S * b : S * b + S],
+                    start=(n == 0),
+                    stop=(n == 5),
                 )
+            if part == 1:
+                t = get(rot, [P, 2, 512], F32, "hT", b, 1)
+                nc.scalar.activation(out=t[:, i, :], in_=pt[:], func=COPY, scale=g_col[:, i : i + 1])
 
-        def dxt_tr(b):
+        def hr(b):
+            return get(rot, [P, J, D], F32, "big", ("h", b), 2)
+
+        def back(b):
             for jj in range(2):
-                t = ps_tr.tile([P, 2, 2, P], F32, name="tr")
-                bank["dxr", b, jj] = t
+                ps = ps_tr.tile([P, 2, 2, P], F32, name="tr")
                 for j2 in range(2):
                     for i in range(2):
                         j = 2 * jj + j2
-                        nc.tensor.transpose(t[:, j2, i, :], hT[b][:, i, P * j : P * j + P], ident[:])
+                        nc.tensor.transpose(
+                            ps[:, j2, i, :], tiles["hT", b][:, i, P * j : P * j + P], ident[:]
+                        )
+                for j2 in range(2):
+                    j = 2 * jj + j2
+                    nc.scalar.activation(
+                        out=hr(b)[:, j, 512:768],
+                        in_=ps[:, j2].rearrange("p i q -> p (i q)"),
+                        func=COPY,
+                        scale=r_sb[:, b, j : j + 1],
+                    )
 
-        def dxt_sc(b, j):
-            if ("h", b) not in big:
-                big["h", b] = rot.tile([P, J, D], F32, name="big", bufs=2)
-            nc.scalar.activation(
-                out=big["h", b][:, j, 512:768],
-                in_=bank["dxr", b, j // 2][:, j % 2].rearrange("p i q -> p (i q)"),
-                func=COPY,
-                scale=r_sb[:, b, j : j + 1],
-            )
-
-        def dxm_mm(b, j):
-            pt = ps_mm.tile([P, 512], F32, name="mm")
-            bank["dxm", b, j] = pt
+        def dxm(b, j, part):
+            pt = get(ps_dx, [P, 512], F32, "dx", ("m", b, j), 2)
             t0 = S * b + P * j
-            for n in range(6):
+            for n in (range(4), range(4, 6))[part]:
                 nc.tensor.matmul_mx(
                     out=pt[:],
                     lhsT=dyf_c[:, n, t0 : t0 + P].bitcast(E5),
@@ -264,24 +279,21 @@ def tile_transformerblock_pa_v_kernel(
                     start=(n == 0),
                     stop=(n == 5),
                 )
+            if part == 1:
+                nc.vector.scalar_tensor_tensor(
+                    out=hr(b)[:, j, 0:512],
+                    in0=pt[:],
+                    scalar=r_sb[:, b, j : j + 1],
+                    in1=g_bc[:, 0:512],
+                    op0=MULT,
+                    op1=MULT,
+                )
 
-        def dx1(b, j):
-            if ("h", b) not in big:
-                big["h", b] = rot.tile([P, J, D], F32, name="big", bufs=2)
-            nc.vector.scalar_tensor_tensor(
-                out=big["h", b][:, j, 0:512],
-                in0=bank["dxm", b, j][:],
-                scalar=r_sb[:, b, j : j + 1],
-                in1=g_bc[:, 0:512],
-                op0=MULT,
-                op1=MULT,
-            )
-
-        def dx2(b, j):
+        def d2(b, j):
             junk = rot.tile([P, D], F32, name="junk", bufs=1)
             nc.vector.scalar_tensor_tensor(
                 out=junk[:],
-                in0=big["h", b][:, j, :],
+                in0=hr(b)[:, j, :],
                 scalar=nr2[:, b, j : j + 1],
                 in1=x_sb[:, b, j, :],
                 op0=MULT,
@@ -289,180 +301,216 @@ def tile_transformerblock_pa_v_kernel(
                 accum_out=c_sb[:, b, j : j + 1],
             )
 
-        def dx3(b, j):
+        def d3(b, j):
             nc.vector.scalar_tensor_tensor(
-                out=big["h", b][:, j, :],
+                out=hr(b)[:, j, :],
                 in0=x_sb[:, b, j, :],
                 scalar=c_sb[:, b, j : j + 1],
-                in1=big["h", b][:, j, :],
+                in1=hr(b)[:, j, :],
                 op0=MULT,
                 op1=ADD,
             )
-
-        def dx_st(b, j):
             dst = out_0[b].rearrange("(p j) d -> p j d", j=J)
-            nc.sync.dma_start(out=dst[:, j], in_=big["h", b][:, j, :])
+            nc.sync.dma_start(out=dst[:, j], in_=hr(b)[:, j, :])
 
         nc.gpsimd.memset(g_row[:], 0.0)
         nc.gpsimd.memset(ones[:], 1.0)
         make_identity(nc, ident[:])
         nc.sync.dma_start(out=g_row[0:1, :], in_=g1.rearrange("(o d) -> o d", o=1))
         nc.sync.dma_start(out=r_sb[:], in_=r.rearrange("b (p j) -> p b j", j=J))
-        load_x(0)
-        load_dy(0, 0)
-        load_x(1)
-        load_dy(0, 1)
-        load_dy(1, 0)
-        load_dy(1, 1)
-        load_w(0)
-        load_w(1)
-        load_w(2)
+        dummy = keep.tile([P, 1], F32, name="dummy")
         nc.vector.memset(dummy[:], 0.0)
         nc.scalar.activation(out=dummy[:], in_=dummy[:], func=COPY)
-
         gp0 = ps_mm.tile([P, 512], F32, name="mm")
         gp1 = ps_mm.tile([P, 512], F32, name="mm")
         nc.tensor.matmul(gp0[:], lhsT=ones[:], rhs=g_row[:, 0:512], start=True, stop=True)
         nc.tensor.matmul(gp1[:, 0:256], lhsT=ones[:], rhs=g_row[:, 512:768], start=True, stop=True)
-        nc.scalar.copy(out=g_bc[:, 0:512], in_=gp0[:])
-        nc.scalar.copy(out=g_bc[:, 512:768], in_=gp1[:, 0:256])
+        nc.vector.tensor_copy(out=g_bc[:, 0:512], in_=gp0[:])
+        nc.vector.tensor_copy(out=g_bc[:, 512:768], in_=gp1[:, 0:256])
         gp2 = ps_tr.tile([P, 2, 2, P], F32, name="tr")
         for i in range(2):
             nc.tensor.transpose(gp2[:, 0, i, :], g_bc[:, 512 + P * i : 640 + P * i], ident[:])
-        nc.vector.tensor_copy(out=g_col[:], in_=gp2[:, 0, :, 0])
         nc.vector.scalar_tensor_tensor(
             out=nr2[:], in0=r_sb[:], scalar=-1.0 / D, in1=r_sb[:], op0=MULT, op1=MULT
         )
-
-        xr(0)
-        tr(0, 0, 0)
-        fe(0, 0, 0)
-        xn(0)
-        xr(1)
-        it(0, 0, 0, nc.vector)
+        nc.vector.tensor_copy(out=g_col[:], in_=gp2[:, 0, :, 0])
+        load_x(0)
+        load_x(1)
+        norm(0, 0)
+        load_dy(0, 0)
+        norm(0, 1)
+        norm(0, 2)
+        norm(1, 1)
         xq(0)
-        tr(0, 0, 1)
-        fe(0, 0, 1)
-        xn(1)
-        qt(0, 0, 0)
-        it(0, 1, 0, nc.vector)
-        xq(1)
-        qf(0, 0, 0)
-        qt(0, 1, 0)
-        tr(0, 1, 0)
-        fe(0, 1, 0)
-        it(0, 0, 1, nc.vector)
+        load_dy(0, 1)
+        norm(1, 0)
+        it(0, 0, 0, 1, V)
+        norm(1, 2)
+        it(0, 0, 1, 1, A)
+        feat(0, 0, 1)
+        load_dy(1, 0)
+        it(0, 0, 0, 0, A)
+        feat(0, 0, 0)
+        it(0, 1, 1, 1, A)
+        it(0, 0, 1, 0, V)
+        it(0, 1, 1, 0, A)
         qf(0, 0, 1)
-        it(0, 1, 1, nc.vector)
+        xq(1)
         qt(0, 0, 1)
-        tr(0, 1, 1)
-        fe(0, 1, 1)
-        qf(0, 1, 0)
+        feat(0, 1, 0)
+        load_w(1)
+        qt(0, 0, 0)
+        it(0, 1, 0, 1, A)
+        it(0, 1, 0, 0, V)
+        qf(0, 0, 0)
+        ps(1, 0, 0, V)
+        feat(1, 0, 0)
+        it(1, 0, 1, 0, V)
         qt(0, 1, 1)
+        it(1, 0, 1, 1, V)
+        load_w(0)
+        ps(1, 0, 1, A)
+        load_dy(1, 1)
         load_dy(2, 0)
+        iw(1, 1, V)
+        dw(0, 6, A)
+        dw(0, 5, A)
+        qt(1, 0, 1)
+        qf(0, 1, 0)
+        iw(0, 0, V)
+        iw(1, 2, V)
+        feat(1, 0, 1)
+        load_w(2)
+        dw(0, 7, A)
+        dw(0, 4, A)
+        iw(0, 2, V)
+        it(1, 1, 1, 1, V)
+        qt(0, 1, 0)
+        iw(1, 0, A)
+        it(1, 1, 1, 0, V)
+        load_w(3)
+        feat(0, 1, 1)
+        it(1, 1, 0, 0, V)
+        dw(0, 0, A)
+        iw(0, 1, V)
+        dw(0, 2, A)
+        ps(2, 0, 0, V)
+        load_w(5)
+        qf(1, 0, 0)
+        qt(1, 1, 1)
+        qw(1)
+        it(1, 1, 0, 1, V)
+        feat(2, 0, 0)
+        qw(0)
+        qt(1, 1, 0)
+        ps(2, 0, 1, V)
+        iw(2, 0, V)
+        ps(1, 1, 0, V)
+        dw(1, 5, A)
+        dw(1, 7, A)
+        iw(3, 2, A)
+        qf(1, 0, 1)
+        dw(1, 6, A)
+        iw(3, 1, V)
+        dw(0, 3, A)
+        iw(2, 2, A)
+        feat(2, 0, 1)
+        it(1, 0, 0, 1, A)
+        iw(3, 0, V)
+        it(1, 0, 0, 0, V)
+        iw(2, 1, V)
+        qw(3)
+        load_w(4)
+        qw(2)
         load_dy(2, 1)
-
-        halves = [(a, b, g) for a in (1, 2) for b in range(B) for g in range(2)]
-        w_iw = {1: 0, 3: 1, 4: 2, 5: 3, 6: 4, 7: 5}
-        prev = (0, 1, 1)
-        pend = None
-        for i, (a, b, g) in enumerate(halves):
-            tr(a, b, g)
-            fe(a, b, g)
-            if a == 1:
-                it(a, b, g, nc.vector)
-            if pend is not None:
-                qw(pend)
-                if pend + 3 < 6:
-                    load_w(pend + 3)
-                pend = None
-            qf(*prev)
-            prev = (a, b, g)
-            if i in w_iw:
-                iw(w_iw[i])
-                pend = w_iw[i]
-            if a == 1:
-                qt(a, b, g)
-            for h in (2 * (i % 4), 2 * (i % 4) + 1):
-                dw_mm(a - 1, h)
-                dw_ev(a - 1, h)
-                dw_st(a - 1, h, nc.scalar if a == 1 else nc.sync)
-        qf(*prev)
-        qw(pend)
-
-        dxt_mm(0)
-        dxt_ev(0)
-        it(2, 0, 0, nc.scalar, 2)
-        dxm_mm(0, 0)
-        dx1(0, 0)
-        dxm_mm(0, 1)
-        dx1(0, 1)
-        dxt_tr(0)
-        dxt_sc(0, 0)
-        dxt_sc(0, 1)
-        dxt_sc(0, 2)
-        dxt_sc(0, 3)
-        it(2, 1, 0, nc.scalar, 2)
-        qt(2, 0, 0)
-        dx2(0, 0)
-        dx2(0, 1)
-        dx3(0, 0)
-        dx_st(0, 0)
-        dx3(0, 1)
-        dx_st(0, 1)
-        qt(2, 1, 0)
-        dxm_mm(0, 2)
-        dx1(0, 2)
-        dxm_mm(0, 3)
-        dx1(0, 3)
-        it(2, 0, 1, nc.scalar, 2)
-        dx2(0, 2)
-        dx2(0, 3)
-        dx3(0, 2)
-        dx_st(0, 2)
-        dx3(0, 3)
-        dx_st(0, 3)
-        for h in (0, 1):
-            dw_mm(2, h)
-            dw_ev(2, h)
-            dw_st(2, h, nc.sync)
-        it(2, 1, 1, nc.scalar, 2)
-        qt(2, 0, 1)
-        dxt_mm(1)
-        dxt_ev(1)
-        dxm_mm(1, 0)
-        dx1(1, 0)
-        dxm_mm(1, 1)
-        dx1(1, 1)
+        ps(1, 1, 1, V)
+        qf(0, 1, 1)
+        iw(5, 0, V)
+        qt(1, 0, 0)
+        dw(1, 4, A)
+        dw(0, 1, A)
+        iw(5, 1, V)
+        feat(1, 1, 0)
+        iw(5, 2, V)
+        dxt(0, 0, 0)
+        qf(2, 0, 1)
+        iw(4, 2, V)
+        dxm(0, 2, 0)
+        iw(4, 0, V)
+        qf(2, 0, 0)
+        qw(5)
+        dw(1, 2, A)
+        iw(4, 1, A)
+        qw(4)
+        dw(1, 0, A)
+        ps(2, 1, 1, V)
+        feat(1, 1, 1)
+        dw(1, 1, V)
+        dw(1, 3, A)
+        ps(2, 1, 0, V)
+        dxt(0, 0, 1)
+        dxm(0, 2, 1)
+        it(2, 1, 1, 0, A)
+        it(2, 1, 1, 1, V)
+        feat(2, 1, 1)
+        qf(1, 1, 0)
+        dxt(0, 1, 0)
+        dxt(0, 1, 1)
         qt(2, 1, 1)
-        dxt_tr(1)
-        for j in range(J):
-            dxt_sc(1, j)
-        dx2(1, 0)
-        dx2(1, 1)
-        dx3(1, 0)
-        dx_st(1, 0)
-        dx3(1, 1)
-        dx_st(1, 1)
-        for h in (2, 3):
-            dw_mm(2, h)
-            dw_ev(2, h)
-            dw_st(2, h, nc.sync)
-        dxm_mm(1, 2)
-        dx1(1, 2)
-        dxm_mm(1, 3)
-        dx1(1, 3)
-        for h in (4, 5):
-            dw_mm(2, h)
-            dw_ev(2, h)
-            dw_st(2, h, nc.sync)
-        dx2(1, 2)
-        dx2(1, 3)
-        dx3(1, 2)
-        dx_st(1, 2)
-        dx3(1, 3)
-        dx_st(1, 3)
-        for h in (6, 7):
-            dw_mm(2, h)
-            dw_ev(2, h)
-            dw_st(2, h, nc.sync)
+        it(2, 0, 0, 1, V)
+        qf(2, 1, 1)
+        feat(2, 1, 0)
+        qf(1, 1, 1)
+        dxm(0, 1, 0)
+        it(2, 1, 0, 1, A)
+        it(2, 1, 0, 0, V)
+        it(2, 0, 0, 0, A)
+        qf(2, 1, 0)
+        back(0)
+        dxm(0, 1, 1)
+        qt(2, 1, 0)
+        qt(2, 0, 0)
+        dxm(0, 0, 0)
+        dxm(0, 0, 1)
+        d2(0, 1)
+        d2(0, 0)
+        it(2, 0, 1, 0, A)
+        dxm(0, 3, 0)
+        dxm(0, 3, 1)
+        d2(0, 2)
+        it(2, 0, 1, 1, A)
+        dw(2, 1, A)
+        d3(0, 0)
+        d3(0, 2)
+        d2(0, 3)
+        dxt(1, 0, 0)
+        dxt(1, 0, 1)
+        dxt(1, 1, 0)
+        d3(0, 1)
+        qt(2, 0, 1)
+        dxt(1, 1, 1)
+        dxm(1, 0, 0)
+        dxm(1, 0, 1)
+        d3(0, 3)
+        back(1)
+        dxm(1, 2, 0)
+        d2(1, 0)
+        dxm(1, 2, 1)
+        dxm(1, 1, 0)
+        d3(1, 0)
+        dxm(1, 1, 1)
+        d2(1, 2)
+        d2(1, 1)
+        dw(2, 0, A)
+        d3(1, 2)
+        dw(2, 7, A)
+        d3(1, 1)
+        dxm(1, 3, 0)
+        dxm(1, 3, 1)
+        dw(2, 6, A)
+        d2(1, 3)
+        d3(1, 3)
+        dw(2, 2, A)
+        dw(2, 4, A)
+        dw(2, 3, V)
+        dw(2, 5, A)

@@ -18,7 +18,6 @@ E = H * DK
 T = B * S
 P = 128
 J = 4
-PRE = (1, 2)
 FLOPS = 2 * 2 * T * 3 * E * D
 
 
@@ -34,9 +33,7 @@ def tile_transformerblock_pa_v_kernel(
     with ExitStack() as ctx:
         keep = ctx.enter_context(tc.tile_pool(name="keep", bufs=1))
         rot = ctx.enter_context(tc.tile_pool(name="rot", bufs=2))
-        ps_tr = ctx.enter_context(tc.psum_pool(name="ps_tr", bufs=2))
-        ps_mm = ctx.enter_context(tc.psum_pool(name="ps_mm", bufs=4))
-        ps_dx = ctx.enter_context(tc.psum_pool(name="ps_dx", bufs=2))
+        psum = ctx.enter_context(tc.psum_pool(name="psum", bufs=8))
         ctx.enter_context(tc.manual_schedule())
 
         ident = keep.tile([P, P], F32, name="ident")
@@ -72,33 +69,37 @@ def tile_transformerblock_pa_v_kernel(
             for lo in range(0, D, step):
                 nc.sync.dma_start(out=x_sb[:, b, :, lo : lo + step], in_=src[:, :, lo : lo + step])
 
-        def dy_raw(a, b):
-            return get(rot, [P, J, E], BF16, "dy_raw", (a, b), 4)
+        def dy_raw(a, b, g):
+            shape = [P, J, 512] if a == 0 else [P, 4, J, DK]
+            return get(rot, shape, BF16, "dy_raw", (a, b, g), 8)
 
-        def load_dy(a, b):
-            if a in PRE:
-                src = grads[a][b].rearrange("h (p j) d -> p h (j d)", j=J)
-                flat = dy_raw(a, b)[:].rearrange("p j f -> p (j f)").rearrange("p (h k) -> p h k", h=H)
-                for g in range(2):
-                    nc.sync.dma_start(out=flat[:, 4 * g : 4 * g + 4], in_=src[:, 4 * g : 4 * g + 4])
-                return
-            src = grads[a][b].rearrange("h (p j) d -> p j h d", j=J)
-            for j in range(J):
+        def load_dy(a, b, g):
+            t = dy_raw(a, b, g)
+            src = grads[a][b][4 * g : 4 * g + 4]
+            if a == 0:
+                src = src.rearrange("h (p j) d -> p j h d", j=J)
+                for j in range(J):
+                    nc.sync.dma_start(
+                        out=t[:, j, :].rearrange("p (h d) -> p h d", d=DK), in_=src[:, j]
+                    )
+            else:
                 nc.sync.dma_start(
-                    out=dy_raw(a, b)[:, j, :].rearrange("p (h d) -> p h d", d=DK), in_=src[:, j]
+                    out=t[:].rearrange("p h j d -> p h (j d)"),
+                    in_=src.rearrange("h (p j) d -> p h (j d)", j=J),
                 )
+
+        def copy(eng, out, in_):
+            if eng is A:
+                nc.scalar.copy(out=out, in_=in_)
+            else:
+                nc.vector.tensor_copy(out=out, in_=in_)
 
         def ps(a, b, g, eng):
             t = get(rot, [P, J, 2, P], F32, "srt", (a, b, g), 2)
-            words = dy_raw(a, b)[:].rearrange("p j f -> p (j f)").bitcast(F32)
-            words = words.rearrange("p (h j w) -> p h j w", h=H, j=J)
+            words = dy_raw(a, b, g)[:].rearrange("p h j d -> p (h j d)").bitcast(F32)
+            words = words.rearrange("p (h j w) -> p j h w", h=4, j=J)
             for u in range(2):
-                o = t[:, :, u, :].rearrange("p j (h q) -> p j h q", h=4)
-                n = words[:, 4 * g : 4 * g + 4, :, u::2].rearrange("p h j q -> p j h q")
-                if eng is A:
-                    nc.scalar.copy(out=o, in_=n)
-                else:
-                    nc.vector.tensor_copy(out=o, in_=n)
+                copy(eng, t[:, :, u, :].rearrange("p j (h q) -> p j h q", h=4), words[:, :, :, u::2])
 
         def w_raw(n):
             return get(rot, [P, J, D], BF16, "w_raw", n, 3)
@@ -115,13 +116,17 @@ def tile_transformerblock_pa_v_kernel(
             lo, hi = 256 * k, 256 * k + 256
             t = get(rot, [P, J, D], F32, "big", ("x", b), 2)
             for j in range(J):
-                nc.scalar.activation(
-                    out=t[:, j, lo:hi], in_=x_sb[:, b, j, lo:hi], func=COPY, scale=r_sb[:, b, j : j + 1]
-                )
+                xs, rs = x_sb[:, b, j, lo:hi], r_sb[:, b, j : j + 1]
+                if b == 0:
+                    nc.scalar.activation(out=t[:, j, lo:hi], in_=xs, func=COPY, scale=rs)
+                else:
+                    nc.gpsimd.tensor_scalar(
+                        out=t[:, j, lo:hi], in0=xs, scalar1=rs, scalar2=0.0, op0=MULT, op1=ADD
+                    )
             nc.vector.tensor_tensor(
                 out=grouped_d(("x", b))[:, lo:hi, :],
                 in0=t[:, :, lo:hi].rearrange("p j d -> p d j"),
-                in1=g_bc[:, lo:hi].unsqueeze(2).to_broadcast([P, hi - lo, J]),
+                in1=gps[k // 2][:, lo % 512 : lo % 512 + 256].unsqueeze(2).to_broadcast([P, 256, J]),
                 op=MULT,
             )
 
@@ -136,23 +141,21 @@ def tile_transformerblock_pa_v_kernel(
             quant_d(xn_c[:, b, :], xn_s[:, b, :], grouped_d(("x", b)))
 
         def feat(a, b, g):
-            words = dy_raw(a, b)[:].rearrange("p j f -> p (j f)").bitcast(F32)
+            if a == 0:
+                words = dy_raw(a, b, g)[:].rearrange("p j f -> p (j f)").bitcast(F32)
+                words = words.rearrange("p (j w u) -> p j u w", j=J, u=2)
+            else:
+                words = tiles["srt", (a, b, g)]
             t = get(rot, [P, 2048], BF16, "gf", (a, b, g), 3, 64)
             out_words = t[:].bitcast(F32)
             for jj in range(2):
-                ps = ps_tr.tile([P, 2, 2, P], F32, name="tr")
+                bank = psum.tile([P, 2, 2, P], F32, name="bank")
                 for j2 in range(2):
                     for u in range(2):
-                        j = 2 * jj + j2
-                        lo = j * (E // 2) + 256 * g
-                        if a in PRE:
-                            src = tiles["srt", (a, b, g)][:, j, u, :]
-                        else:
-                            src = words[:, lo + u : lo + 256 : 2]
-                        nc.tensor.transpose(ps[:, j2, u, :], src, ident[:])
+                        nc.tensor.transpose(bank[:, j2, u, :], words[:, 2 * jj + j2, u, :], ident[:])
                 nc.scalar.copy(
                     out=out_words[:, 512 * jj : 512 * jj + 512].rearrange("p (j q u) -> p j q u", j=2, u=2),
-                    in_=ps[:].rearrange("p j u q -> p j q u"),
+                    in_=bank[:].rearrange("p j u q -> p j q u"),
                 )
 
         def qf(a, b, g):
@@ -166,25 +169,20 @@ def tile_transformerblock_pa_v_kernel(
         def interleave(eng, out, in_):
             o = out.rearrange("p (c i) j -> p c j i", i=4)
             n = in_.rearrange("p j (c i) -> p c j i", i=4)
-            if eng is A:
-                nc.scalar.copy(out=o, in_=n)
-            else:
-                nc.vector.tensor_copy(out=o, in_=n)
+            copy(eng, o, n)
 
         def it(a, b, g, k, eng):
             t = get(rot, [P, 512, J], BF16, "gt", (a, b, g), 3, 64)
-            lo = 256 * k
-            if a in PRE:
-                flat = dy_raw(a, b)[:].rearrange("p j f -> p (j f)")
-                raw = flat.rearrange("p (h j d) -> p h j d", h=H, j=J)[:, 4 * g + 2 * k : 4 * g + 2 * k + 2]
-                o = t[:, lo : lo + 256, :].rearrange("p (h c i) j -> p h c j i", h=2, i=4)
-                n = raw.rearrange("p h j (c i) -> p h c j i", i=4)
-                if eng is A:
-                    nc.scalar.copy(out=o, in_=n)
-                else:
-                    nc.vector.tensor_copy(out=o, in_=n)
-                return
-            interleave(eng, t[:, lo : lo + 256, :], dy_raw(a, b)[:, :, 512 * g + lo : 512 * g + lo + 256])
+            o = t[:, 256 * k : 256 * k + 256, :]
+            raw = dy_raw(a, b, g)
+            if a == 0:
+                interleave(eng, o, raw[:, :, 256 * k : 256 * k + 256])
+            else:
+                copy(
+                    eng,
+                    o.rearrange("p (h c i) j -> p h c j i", h=2, i=4),
+                    raw[:, 2 * k : 2 * k + 2].rearrange("p h j (c i) -> p h c j i", i=4),
+                )
 
         def dyt(a):
             return (
@@ -207,14 +205,14 @@ def tile_transformerblock_pa_v_kernel(
         def qw(n):
             quant_d(w_c[:, n, :], w_s[:, n, :], grouped_d(n))
 
-        def dw(a, h, eng):
+        def dw(a, h, engines):
             codes, scales = dyt(a)
-            p0 = ps_mm.tile([P, 512], F32, name="mm")
-            p1 = ps_mm.tile([P, 512], F32, name="mm")
-            for b in range(B):
-                for pt, lo in ((p0, 0), (p1, 256)):
+            t = rot.tile([P, D], F32, name="res", bufs=4)
+            for lo, cut, eng in ((0, 0, engines[0]), (256, 256, engines[1])):
+                bank = psum.tile([P, 512], F32, name="bank")
+                for b in range(B):
                     nc.tensor.matmul_mx(
-                        out=pt[:],
+                        out=bank[:],
                         lhsT=codes[:, b, P * h : P * h + P].bitcast(E5),
                         lhsT_scale=scales[:, b, P * h : P * h + P],
                         rhs=xn_c[:, b, lo : lo + 512].bitcast(E4),
@@ -222,14 +220,11 @@ def tile_transformerblock_pa_v_kernel(
                         start=(b == 0),
                         stop=(b == B - 1),
                     )
-            t = rot.tile([P, D], F32, name="res", bufs=4)
-            move = nc.scalar.copy if eng is A else nc.vector.tensor_copy
-            move(out=t[:, 0:512], in_=p0[:])
-            move(out=t[:, 512:768], in_=p1[:, 256:512])
+                copy(eng, t[:, lo + cut : lo + 512], bank[:, cut:512])
             nc.sync.dma_start(out=w_outs[a][P * h : P * h + P, :], in_=t[:])
 
         def dxt(b, i, part):
-            pt = get(ps_dx, [P, 512], F32, "dx", ("t", b, i), 2)
+            pt = get(psum, [P, 512], F32, "bank", ("t", b, i), None)
             d0 = 512 + P * i
             for n in (range(4), range(4, 6))[part]:
                 nc.tensor.matmul_mx(
@@ -250,24 +245,24 @@ def tile_transformerblock_pa_v_kernel(
 
         def back(b):
             for jj in range(2):
-                ps = ps_tr.tile([P, 2, 2, P], F32, name="tr")
+                bank = psum.tile([P, 2, 2, P], F32, name="bank")
                 for j2 in range(2):
                     for i in range(2):
                         j = 2 * jj + j2
                         nc.tensor.transpose(
-                            ps[:, j2, i, :], tiles["hT", b][:, i, P * j : P * j + P], ident[:]
+                            bank[:, j2, i, :], tiles["hT", b][:, i, P * j : P * j + P], ident[:]
                         )
                 for j2 in range(2):
                     j = 2 * jj + j2
                     nc.scalar.activation(
                         out=hr(b)[:, j, 512:768],
-                        in_=ps[:, j2].rearrange("p i q -> p (i q)"),
+                        in_=bank[:, j2].rearrange("p i q -> p (i q)"),
                         func=COPY,
                         scale=r_sb[:, b, j : j + 1],
                     )
 
         def dxm(b, j, part):
-            pt = get(ps_dx, [P, 512], F32, "dx", ("m", b, j), 2)
+            pt = get(psum, [P, 512], F32, "bank", ("m", b, j), None)
             t0 = S * b + P * j
             for n in (range(4), range(4, 6))[part]:
                 nc.tensor.matmul_mx(
@@ -321,13 +316,14 @@ def tile_transformerblock_pa_v_kernel(
         dummy = keep.tile([P, 1], F32, name="dummy")
         nc.vector.memset(dummy[:], 0.0)
         nc.scalar.activation(out=dummy[:], in_=dummy[:], func=COPY)
-        gp0 = ps_mm.tile([P, 512], F32, name="mm")
-        gp1 = ps_mm.tile([P, 512], F32, name="mm")
+        gp0 = psum.tile([P, 512], F32, name="bank")
+        gp1 = psum.tile([P, 512], F32, name="bank")
+        gps = (gp0, gp1)
         nc.tensor.matmul(gp0[:], lhsT=ones[:], rhs=g_row[:, 0:512], start=True, stop=True)
         nc.tensor.matmul(gp1[:, 0:256], lhsT=ones[:], rhs=g_row[:, 512:768], start=True, stop=True)
         nc.vector.tensor_copy(out=g_bc[:, 0:512], in_=gp0[:])
         nc.vector.tensor_copy(out=g_bc[:, 512:768], in_=gp1[:, 0:256])
-        gp2 = ps_tr.tile([P, 2, 2, P], F32, name="tr")
+        gp2 = psum.tile([P, 2, 2, P], F32, name="bank")
         for i in range(2):
             nc.tensor.transpose(gp2[:, 0, i, :], g_bc[:, 512 + P * i : 640 + P * i], ident[:])
         nc.vector.scalar_tensor_tensor(
@@ -335,182 +331,188 @@ def tile_transformerblock_pa_v_kernel(
         )
         nc.vector.tensor_copy(out=g_col[:], in_=gp2[:, 0, :, 0])
         load_x(0)
-        load_x(1)
+        load_dy(1, 1, 1)
         norm(0, 0)
-        load_dy(0, 0)
         norm(0, 1)
-        norm(0, 2)
-        norm(1, 1)
-        xq(0)
-        load_dy(0, 1)
-        norm(1, 0)
-        it(0, 0, 0, 1, V)
-        norm(1, 2)
-        it(0, 0, 1, 1, A)
-        feat(0, 0, 1)
-        load_dy(1, 0)
-        it(0, 0, 0, 0, A)
-        feat(0, 0, 0)
-        it(0, 1, 1, 1, A)
-        it(0, 0, 1, 0, V)
-        it(0, 1, 1, 0, A)
-        qf(0, 0, 1)
-        xq(1)
-        qt(0, 0, 1)
-        feat(0, 1, 0)
-        load_w(1)
-        qt(0, 0, 0)
-        it(0, 1, 0, 1, A)
-        it(0, 1, 0, 0, V)
-        qf(0, 0, 0)
-        ps(1, 0, 0, V)
-        feat(1, 0, 0)
-        it(1, 0, 1, 0, V)
-        qt(0, 1, 1)
-        it(1, 0, 1, 1, V)
-        load_w(0)
-        ps(1, 0, 1, A)
-        load_dy(1, 1)
-        load_dy(2, 0)
-        iw(1, 1, V)
-        dw(0, 6, A)
-        dw(0, 5, A)
-        qt(1, 0, 1)
-        qf(0, 1, 0)
-        iw(0, 0, V)
-        iw(1, 2, V)
-        feat(1, 0, 1)
-        load_w(2)
-        dw(0, 7, A)
-        dw(0, 4, A)
-        iw(0, 2, V)
-        it(1, 1, 1, 1, V)
-        qt(0, 1, 0)
-        iw(1, 0, A)
-        it(1, 1, 1, 0, V)
-        load_w(3)
-        feat(0, 1, 1)
-        it(1, 1, 0, 0, V)
-        dw(0, 0, A)
-        iw(0, 1, V)
-        dw(0, 2, A)
-        ps(2, 0, 0, V)
-        load_w(5)
-        qf(1, 0, 0)
-        qt(1, 1, 1)
-        qw(1)
-        it(1, 1, 0, 1, V)
-        feat(2, 0, 0)
-        qw(0)
-        qt(1, 1, 0)
-        ps(2, 0, 1, V)
-        iw(2, 0, V)
-        ps(1, 1, 0, V)
-        dw(1, 5, A)
-        dw(1, 7, A)
-        iw(3, 2, A)
-        qf(1, 0, 1)
-        dw(1, 6, A)
-        iw(3, 1, V)
-        dw(0, 3, A)
-        iw(2, 2, A)
-        feat(2, 0, 1)
-        it(1, 0, 0, 1, A)
-        iw(3, 0, V)
-        it(1, 0, 0, 0, V)
-        iw(2, 1, V)
-        qw(3)
-        load_w(4)
-        qw(2)
-        load_dy(2, 1)
+        load_dy(1, 0, 0)
         ps(1, 1, 1, V)
-        qf(0, 1, 1)
-        iw(5, 0, V)
-        qt(1, 0, 0)
-        dw(1, 4, A)
-        dw(0, 1, A)
-        iw(5, 1, V)
-        feat(1, 1, 0)
-        iw(5, 2, V)
-        dxt(0, 0, 0)
-        qf(2, 0, 1)
-        iw(4, 2, V)
-        dxm(0, 2, 0)
-        iw(4, 0, V)
-        qf(2, 0, 0)
-        qw(5)
-        dw(1, 2, A)
-        iw(4, 1, A)
-        qw(4)
-        dw(1, 0, A)
-        ps(2, 1, 1, V)
+        it(1, 1, 1, 1, V)
+        norm(0, 2)
+        it(1, 1, 1, 0, A)
+        qt(1, 1, 1)
+        xq(0)
+        ps(1, 0, 0, A)
+        load_x(1)
         feat(1, 1, 1)
-        dw(1, 1, V)
-        dw(1, 3, A)
-        ps(2, 1, 0, V)
-        dxt(0, 0, 1)
-        dxm(0, 2, 1)
-        it(2, 1, 1, 0, A)
-        it(2, 1, 1, 1, V)
-        feat(2, 1, 1)
-        qf(1, 1, 0)
-        dxt(0, 1, 0)
-        dxt(0, 1, 1)
-        qt(2, 1, 1)
-        it(2, 0, 0, 1, V)
-        qf(2, 1, 1)
-        feat(2, 1, 0)
+        load_dy(1, 0, 1)
         qf(1, 1, 1)
+        norm(1, 1)
+        norm(1, 2)
+        feat(1, 0, 0)
+        load_w(2)
+        load_dy(0, 0, 1)
+        it(1, 0, 1, 0, V)
+        norm(1, 0)
+        ps(1, 0, 1, A)
+        load_dy(2, 0, 0)
+        it(1, 0, 1, 1, A)
+        qt(1, 0, 1)
+        iw(2, 1, A)
+        load_dy(1, 1, 0)
+        feat(1, 0, 1)
+        load_dy(0, 0, 0)
+        load_dy(2, 0, 1)
+        load_w(1)
+        xq(1)
+        iw(2, 2, V)
+        iw(2, 0, V)
+        load_dy(0, 1, 0)
+        it(1, 0, 0, 0, A)
+        feat(0, 0, 1)
+        qf(1, 0, 0)
+        ps(2, 0, 0, V)
+        dw(1, 7, (A, A))
+        it(1, 1, 0, 1, A)
+        load_w(0)
+        qf(0, 0, 1)
+        dw(1, 5, (A, A))
+        qf(1, 0, 1)
+        it(1, 0, 0, 1, V)
+        it(1, 1, 0, 0, V)
+        feat(0, 0, 0)
+        load_w(3)
+        load_dy(0, 1, 1)
+        feat(2, 0, 0)
+        qt(1, 0, 0)
+        ps(2, 0, 1, V)
+        qt(1, 1, 0)
+        iw(1, 2, V)
+        qf(2, 0, 0)
+        dw(1, 6, (A, A))
+        dw(1, 4, (A, V))
+        qf(0, 0, 0)
+        qw(2)
+        ps(1, 1, 0, V)
+        iw(1, 1, A)
+        iw(1, 0, V)
+        iw(0, 0, V)
+        qw(1)
+        feat(2, 0, 1)
+        dw(1, 2, (A, A))
+        load_w(5)
+        iw(0, 2, A)
+        iw(0, 1, V)
+        feat(0, 1, 0)
+        iw(3, 0, V)
+        load_w(4)
+        iw(3, 1, V)
+        qw(0)
+        dw(1, 0, (A, A))
+        iw(3, 2, A)
+        qw(3)
+        feat(1, 1, 0)
+        it(0, 1, 1, 1, A)
+        qf(2, 0, 1)
+        it(0, 0, 1, 0, V)
+        dw(1, 3, (A, V))
+        it(0, 1, 1, 0, V)
+        feat(0, 1, 1)
+        it(0, 0, 1, 1, V)
+        qt(0, 1, 1)
+        dw(1, 1, (A, A))
+        load_dy(2, 1, 0)
+        dxt(0, 0, 0)
+        iw(5, 1, A)
+        load_dy(2, 1, 1)
+        iw(4, 1, A)
+        qt(0, 0, 1)
+        iw(5, 0, V)
+        dxm(0, 0, 0)
+        dxm(0, 2, 0)
+        iw(5, 2, V)
+        dxt(0, 1, 0)
+        iw(4, 0, V)
+        dw(0, 4, (A, A))
+        dw(0, 6, (A, A))
+        iw(4, 2, V)
+        qf(1, 1, 0)
+        qw(4)
+        qw(5)
+        dw(0, 5, (A, A))
+        dw(0, 7, (A, A))
+        it(0, 0, 0, 0, V)
+        dxt(0, 0, 1)
+        ps(2, 1, 0, V)
+        ps(2, 1, 1, V)
+        it(0, 0, 0, 1, V)
+        it(0, 1, 0, 1, A)
+        dxt(0, 1, 1)
+        it(0, 1, 0, 0, A)
+        dxm(0, 0, 1)
+        dxm(0, 2, 1)
         dxm(0, 1, 0)
-        it(2, 1, 0, 1, A)
-        it(2, 1, 0, 0, V)
+        qf(0, 1, 0)
+        dxm(0, 1, 1)
+        qt(0, 0, 0)
+        feat(2, 1, 1)
+        feat(2, 1, 0)
+        back(0)
+        qt(0, 1, 0)
+        dw(0, 1, (A, A))
+        qf(0, 1, 1)
+        dw(0, 2, (A, A))
+        it(2, 1, 1, 1, V)
         it(2, 0, 0, 0, A)
         qf(2, 1, 0)
-        back(0)
-        dxm(0, 1, 1)
-        qt(2, 1, 0)
-        qt(2, 0, 0)
-        dxm(0, 0, 0)
-        dxm(0, 0, 1)
-        d2(0, 1)
+        qf(2, 1, 1)
         d2(0, 0)
-        it(2, 0, 1, 0, A)
-        dxm(0, 3, 0)
-        dxm(0, 3, 1)
+        d2(0, 1)
         d2(0, 2)
-        it(2, 0, 1, 1, A)
-        dw(2, 1, A)
-        d3(0, 0)
-        d3(0, 2)
-        d2(0, 3)
-        dxt(1, 0, 0)
-        dxt(1, 0, 1)
-        dxt(1, 1, 0)
         d3(0, 1)
-        qt(2, 0, 1)
+        it(2, 0, 0, 1, A)
+        dxm(0, 3, 0)
+        dw(0, 0, (A, A))
+        d3(0, 2)
+        qt(2, 0, 0)
+        dxm(0, 3, 1)
+        dxm(1, 1, 0)
+        dxm(1, 1, 1)
+        it(2, 1, 0, 0, A)
+        it(2, 1, 0, 1, V)
+        dxt(1, 0, 0)
+        d2(0, 3)
+        dxt(1, 1, 0)
+        it(2, 1, 1, 0, A)
+        qt(2, 1, 1)
+        dxt(1, 0, 1)
+        qt(2, 1, 0)
         dxt(1, 1, 1)
         dxm(1, 0, 0)
+        d3(0, 0)
+        it(2, 0, 1, 1, A)
         dxm(1, 0, 1)
-        d3(0, 3)
         back(1)
-        dxm(1, 2, 0)
-        d2(1, 0)
-        dxm(1, 2, 1)
-        dxm(1, 1, 0)
-        d3(1, 0)
-        dxm(1, 1, 1)
-        d2(1, 2)
-        d2(1, 1)
-        dw(2, 0, A)
-        d3(1, 2)
-        dw(2, 7, A)
-        d3(1, 1)
+        it(2, 0, 1, 0, A)
+        d3(0, 3)
         dxm(1, 3, 0)
+        d2(1, 0)
+        d2(1, 1)
+        dw(2, 3, (A, A))
+        d3(1, 0)
         dxm(1, 3, 1)
-        dw(2, 6, A)
+        dw(0, 3, (A, A))
+        dw(2, 2, (A, A))
+        qt(2, 0, 1)
         d2(1, 3)
+        d3(1, 1)
         d3(1, 3)
-        dw(2, 2, A)
-        dw(2, 4, A)
-        dw(2, 3, V)
-        dw(2, 5, A)
+        dxm(1, 2, 0)
+        dxm(1, 2, 1)
+        dw(2, 7, (A, A))
+        dw(2, 4, (A, A))
+        d2(1, 2)
+        d3(1, 2)
+        dw(2, 1, (A, A))
+        dw(2, 6, (A, V))
+        dw(2, 0, (A, V))
+        dw(2, 5, (V, A))

@@ -18,6 +18,7 @@ E = H * DK
 T = B * S
 P = 128
 J = 4
+SORTED = ((2, 0), (2, 1))
 FLOPS = 2 * 2 * T * 3 * E * D
 
 
@@ -70,13 +71,13 @@ def tile_transformerblock_pa_v_kernel(
                 nc.sync.dma_start(out=x_sb[:, b, :, lo : lo + step], in_=src[:, :, lo : lo + step])
 
         def dy_raw(a, b, g):
-            shape = [P, J, 512] if a == 0 else [P, 4, J, DK]
+            shape = [P, 4, J, DK] if (a, b) in SORTED else [P, J, 512]
             return get(rot, shape, BF16, "dy_raw", (a, b, g), 8)
 
         def load_dy(a, b, g):
             t = dy_raw(a, b, g)
             src = grads[a][b][4 * g : 4 * g + 4]
-            if a == 0:
+            if (a, b) not in SORTED:
                 src = src.rearrange("h (p j) d -> p j h d", j=J)
                 for j in range(J):
                     nc.sync.dma_start(
@@ -117,12 +118,7 @@ def tile_transformerblock_pa_v_kernel(
             t = get(rot, [P, J, D], F32, "big", ("x", b), 2)
             for j in range(J):
                 xs, rs = x_sb[:, b, j, lo:hi], r_sb[:, b, j : j + 1]
-                if b == 0:
-                    nc.scalar.activation(out=t[:, j, lo:hi], in_=xs, func=COPY, scale=rs)
-                else:
-                    nc.gpsimd.tensor_scalar(
-                        out=t[:, j, lo:hi], in0=xs, scalar1=rs, scalar2=0.0, op0=MULT, op1=ADD
-                    )
+                nc.scalar.activation(out=t[:, j, lo:hi], in_=xs, func=COPY, scale=rs)
             nc.vector.tensor_tensor(
                 out=grouped_d(("x", b))[:, lo:hi, :],
                 in0=t[:, :, lo:hi].rearrange("p j d -> p d j"),
@@ -141,7 +137,7 @@ def tile_transformerblock_pa_v_kernel(
             quant_d(xn_c[:, b, :], xn_s[:, b, :], grouped_d(("x", b)))
 
         def feat(a, b, g):
-            if a == 0:
+            if (a, b) not in SORTED:
                 words = dy_raw(a, b, g)[:].rearrange("p j f -> p (j f)").bitcast(F32)
                 words = words.rearrange("p (j w u) -> p j u w", j=J, u=2)
             else:
@@ -175,7 +171,7 @@ def tile_transformerblock_pa_v_kernel(
             t = get(rot, [P, 512, J], BF16, "gt", (a, b, g), 3, 64)
             o = t[:, 256 * k : 256 * k + 256, :]
             raw = dy_raw(a, b, g)
-            if a == 0:
+            if (a, b) not in SORTED:
                 interleave(eng, o, raw[:, :, 256 * k : 256 * k + 256])
             else:
                 copy(
@@ -330,189 +326,185 @@ def tile_transformerblock_pa_v_kernel(
             out=nr2[:], in0=r_sb[:], scalar=-1.0 / D, in1=r_sb[:], op0=MULT, op1=MULT
         )
         nc.vector.tensor_copy(out=g_col[:], in_=gp2[:, 0, :, 0])
-        load_x(0)
+        load_x(1)
         load_dy(1, 1, 1)
-        norm(0, 0)
-        norm(0, 1)
-        load_dy(1, 0, 0)
-        ps(1, 1, 1, V)
+        norm(1, 2)
         it(1, 1, 1, 1, V)
+        load_dy(1, 0, 1)
+        it(1, 1, 1, 0, V)
+        load_x(0)
+        load_dy(1, 0, 0)
+        norm(1, 1)
+        norm(1, 0)
+        it(1, 0, 1, 1, V)
+        feat(1, 1, 1)
+        xq(1)
+        it(1, 0, 1, 0, A)
+        norm(0, 1)
+        load_dy(0, 1, 1)
+        norm(0, 0)
+        qt(1, 0, 1)
         norm(0, 2)
-        it(1, 1, 1, 0, A)
+        feat(1, 0, 1)
         qt(1, 1, 1)
         xq(0)
-        ps(1, 0, 0, A)
-        load_x(1)
-        feat(1, 1, 1)
-        load_dy(1, 0, 1)
-        qf(1, 1, 1)
-        norm(1, 1)
-        norm(1, 2)
-        feat(1, 0, 0)
-        load_w(2)
-        load_dy(0, 0, 1)
-        it(1, 0, 1, 0, V)
-        norm(1, 0)
-        ps(1, 0, 1, A)
-        load_dy(2, 0, 0)
-        it(1, 0, 1, 1, A)
-        qt(1, 0, 1)
-        iw(2, 1, A)
         load_dy(1, 1, 0)
-        feat(1, 0, 1)
-        load_dy(0, 0, 0)
-        load_dy(2, 0, 1)
-        load_w(1)
-        xq(1)
-        iw(2, 2, V)
-        iw(2, 0, V)
-        load_dy(0, 1, 0)
+        feat(1, 0, 0)
         it(1, 0, 0, 0, A)
-        feat(0, 0, 1)
+        it(1, 0, 0, 1, A)
+        it(1, 1, 0, 1, V)
+        load_dy(0, 0, 1)
+        load_w(2)
+        qf(1, 1, 1)
         qf(1, 0, 0)
-        ps(2, 0, 0, V)
-        dw(1, 7, (A, A))
-        it(1, 1, 0, 1, A)
-        load_w(0)
-        qf(0, 0, 1)
-        dw(1, 5, (A, A))
-        qf(1, 0, 1)
-        it(1, 0, 0, 1, V)
-        it(1, 1, 0, 0, V)
-        feat(0, 0, 0)
-        load_w(3)
-        load_dy(0, 1, 1)
-        feat(2, 0, 0)
+        load_w(1)
         qt(1, 0, 0)
-        ps(2, 0, 1, V)
+        it(1, 1, 0, 0, A)
+        load_dy(0, 0, 0)
+        qf(1, 0, 1)
         qt(1, 1, 0)
-        iw(1, 2, V)
-        qf(2, 0, 0)
-        dw(1, 6, (A, A))
-        dw(1, 4, (A, V))
-        qf(0, 0, 0)
-        qw(2)
-        ps(1, 1, 0, V)
-        iw(1, 1, A)
-        iw(1, 0, V)
-        iw(0, 0, V)
-        qw(1)
-        feat(2, 0, 1)
-        dw(1, 2, (A, A))
-        load_w(5)
-        iw(0, 2, A)
-        iw(0, 1, V)
-        feat(0, 1, 0)
-        iw(3, 0, V)
-        load_w(4)
-        iw(3, 1, V)
-        qw(0)
-        dw(1, 0, (A, A))
-        iw(3, 2, A)
-        qw(3)
-        feat(1, 1, 0)
-        it(0, 1, 1, 1, A)
-        qf(2, 0, 1)
-        it(0, 0, 1, 0, V)
-        dw(1, 3, (A, V))
-        it(0, 1, 1, 0, V)
         feat(0, 1, 1)
+        load_dy(2, 0, 0)
+        feat(1, 1, 0)
+        iw(2, 2, V)
+        load_w(3)
+        dw(1, 4, (V, A))
+        load_dy(0, 1, 0)
+        iw(2, 0, V)
+        dw(1, 5, (A, A))
+        it(0, 1, 1, 1, A)
         it(0, 0, 1, 1, V)
-        qt(0, 1, 1)
-        dw(1, 1, (A, A))
-        load_dy(2, 1, 0)
-        dxt(0, 0, 0)
-        iw(5, 1, A)
-        load_dy(2, 1, 1)
-        iw(4, 1, A)
-        qt(0, 0, 1)
-        iw(5, 0, V)
-        dxm(0, 0, 0)
-        dxm(0, 2, 0)
-        iw(5, 2, V)
-        dxt(0, 1, 0)
-        iw(4, 0, V)
-        dw(0, 4, (A, A))
-        dw(0, 6, (A, A))
-        iw(4, 2, V)
+        iw(2, 1, A)
+        dw(1, 3, (A, V))
+        dw(1, 0, (A, A))
+        it(0, 1, 1, 0, V)
+        it(0, 0, 1, 0, A)
         qf(1, 1, 0)
-        qw(4)
-        qw(5)
-        dw(0, 5, (A, A))
+        iw(1, 2, V)
+        qw(2)
+        load_w(0)
+        feat(0, 0, 0)
+        qt(0, 1, 1)
+        dw(1, 7, (A, V))
+        iw(1, 1, V)
+        load_dy(2, 0, 1)
+        iw(3, 2, V)
+        qf(0, 1, 1)
+        ps(2, 0, 0, V)
+        feat(0, 0, 1)
+        iw(1, 0, V)
+        dw(1, 2, (V, A))
+        iw(3, 1, A)
+        load_w(4)
+        qt(0, 0, 1)
+        dw(1, 6, (V, A))
+        iw(3, 0, V)
+        dw(1, 1, (A, V))
+        qf(0, 0, 1)
+        load_w(5)
+        load_dy(2, 1, 1)
+        qw(1)
+        qw(3)
+        feat(2, 0, 0)
+        load_dy(2, 1, 0)
+        iw(0, 2, V)
+        iw(0, 0, A)
+        qf(0, 0, 0)
+        ps(2, 0, 1, V)
         dw(0, 7, (A, A))
-        it(0, 0, 0, 0, V)
-        dxt(0, 0, 1)
-        ps(2, 1, 0, V)
-        ps(2, 1, 1, V)
-        it(0, 0, 0, 1, V)
-        it(0, 1, 0, 1, A)
-        dxt(0, 1, 1)
-        it(0, 1, 0, 0, A)
-        dxm(0, 0, 1)
-        dxm(0, 2, 1)
+        iw(0, 1, A)
+        qw(0)
+        iw(4, 1, V)
+        dw(0, 4, (A, A))
+        feat(0, 1, 0)
+        dw(0, 5, (A, A))
+        dw(0, 6, (A, A))
+        iw(4, 0, V)
+        iw(4, 2, V)
+        qf(2, 0, 0)
+        qw(4)
+        feat(2, 0, 1)
         dxm(0, 1, 0)
+        iw(5, 0, A)
+        iw(5, 1, V)
+        dxt(0, 1, 0)
+        dxm(0, 3, 0)
+        it(2, 0, 0, 1, A)
+        iw(5, 2, V)
+        qf(2, 0, 1)
+        qw(5)
+        it(2, 1, 0, 1, A)
+        it(2, 1, 0, 0, V)
+        dxm(0, 2, 0)
+        ps(2, 1, 1, V)
+        dxt(0, 0, 0)
+        it(2, 0, 0, 0, A)
+        dxm(0, 0, 0)
+        dxt(0, 1, 1)
         qf(0, 1, 0)
+        dxt(0, 0, 1)
+        qt(2, 1, 0)
+        dxm(0, 2, 1)
         dxm(0, 1, 1)
-        qt(0, 0, 0)
+        dxm(0, 3, 1)
+        ps(2, 1, 0, A)
+        dxm(0, 0, 1)
+        qt(2, 0, 0)
+        back(0)
         feat(2, 1, 1)
         feat(2, 1, 0)
-        back(0)
-        qt(0, 1, 0)
-        dw(0, 1, (A, A))
-        qf(0, 1, 1)
-        dw(0, 2, (A, A))
-        it(2, 1, 1, 1, V)
-        it(2, 0, 0, 0, A)
-        qf(2, 1, 0)
-        qf(2, 1, 1)
-        d2(0, 0)
+        it(0, 1, 0, 1, V)
         d2(0, 1)
         d2(0, 2)
-        d3(0, 1)
-        it(2, 0, 0, 1, A)
-        dxm(0, 3, 0)
-        dw(0, 0, (A, A))
-        d3(0, 2)
-        qt(2, 0, 0)
-        dxm(0, 3, 1)
-        dxm(1, 1, 0)
-        dxm(1, 1, 1)
-        it(2, 1, 0, 0, A)
-        it(2, 1, 0, 1, V)
+        qf(2, 1, 1)
+        dw(2, 0, (A, A))
+        d2(0, 0)
         dxt(1, 0, 0)
+        it(2, 0, 1, 0, V)
+        qf(2, 1, 0)
+        it(0, 1, 0, 0, A)
+        d3(0, 1)
+        d3(0, 0)
+        dw(2, 1, (A, A))
+        it(0, 0, 0, 0, A)
+        qt(0, 1, 0)
+        d3(0, 2)
+        it(0, 0, 0, 1, A)
+        dxm(1, 2, 0)
         d2(0, 3)
         dxt(1, 1, 0)
-        it(2, 1, 1, 0, A)
-        qt(2, 1, 1)
         dxt(1, 0, 1)
-        qt(2, 1, 0)
+        dxm(1, 2, 1)
+        qt(0, 0, 0)
         dxt(1, 1, 1)
-        dxm(1, 0, 0)
-        d3(0, 0)
-        it(2, 0, 1, 1, A)
-        dxm(1, 0, 1)
-        back(1)
-        it(2, 0, 1, 0, A)
         d3(0, 3)
-        dxm(1, 3, 0)
+        dxm(1, 0, 0)
+        dxm(1, 0, 1)
+        it(2, 0, 1, 1, A)
+        back(1)
+        dw(2, 2, (A, A))
+        d2(1, 2)
+        dw(0, 0, (A, A))
+        dxm(1, 1, 0)
+        it(2, 1, 1, 0, A)
+        it(2, 1, 1, 1, A)
         d2(1, 0)
+        d3(1, 2)
+        dxm(1, 1, 1)
+        qt(2, 0, 1)
         d2(1, 1)
-        dw(2, 3, (A, A))
+        dw(0, 3, (A, A))
+        dw(0, 2, (A, A))
+        qt(2, 1, 1)
+        d3(1, 1)
+        dxm(1, 3, 0)
         d3(1, 0)
         dxm(1, 3, 1)
-        dw(0, 3, (A, A))
-        dw(2, 2, (A, A))
-        qt(2, 0, 1)
-        d2(1, 3)
-        d3(1, 1)
-        d3(1, 3)
-        dxm(1, 2, 0)
-        dxm(1, 2, 1)
-        dw(2, 7, (A, A))
+        dw(2, 5, (A, A))
         dw(2, 4, (A, A))
-        d2(1, 2)
-        d3(1, 2)
-        dw(2, 1, (A, A))
+        d2(1, 3)
+        d3(1, 3)
+        dw(2, 7, (V, V))
         dw(2, 6, (A, V))
-        dw(2, 0, (A, V))
-        dw(2, 5, (V, A))
+        dw(2, 3, (V, V))
+        dw(0, 1, (V, A))

@@ -18,7 +18,7 @@ E = H * DK
 T = B * S
 P = 128
 J = 4
-SORTED = ((2, 0), (2, 1))
+SORTED = ((1, 0), (1, 1), (2, 0), (2, 1))
 FLOPS = 2 * 2 * T * 3 * E * D
 
 
@@ -326,185 +326,189 @@ def tile_transformerblock_pa_v_kernel(
             out=nr2[:], in0=r_sb[:], scalar=-1.0 / D, in1=r_sb[:], op0=MULT, op1=MULT
         )
         nc.vector.tensor_copy(out=g_col[:], in_=gp2[:, 0, :, 0])
-        load_x(1)
-        load_dy(1, 1, 1)
-        norm(1, 2)
-        it(1, 1, 1, 1, V)
-        load_dy(1, 0, 1)
-        it(1, 1, 1, 0, V)
         load_x(0)
+        norm(0, 0)
+        load_dy(1, 1, 0)
         load_dy(1, 0, 0)
+        load_x(1)
+        load_dy(0, 0, 0)
+        norm(0, 1)
+        it(1, 1, 0, 1, V)
+        norm(0, 2)
+        ps(1, 1, 0, A)
+        it(1, 0, 0, 0, V)
+        xq(0)
+        load_dy(0, 1, 0)
+        load_dy(1, 0, 1)
+        ps(1, 0, 0, V)
+        load_dy(1, 1, 1)
+        it(1, 1, 0, 0, A)
+        qt(1, 1, 0)
+        feat(1, 1, 0)
+        qf(1, 1, 0)
+        norm(1, 2)
         norm(1, 1)
         norm(1, 0)
-        it(1, 0, 1, 1, V)
-        feat(1, 1, 1)
-        xq(1)
-        it(1, 0, 1, 0, A)
-        norm(0, 1)
-        load_dy(0, 1, 1)
-        norm(0, 0)
-        qt(1, 0, 1)
-        norm(0, 2)
-        feat(1, 0, 1)
-        qt(1, 1, 1)
-        xq(0)
-        load_dy(1, 1, 0)
-        feat(1, 0, 0)
-        it(1, 0, 0, 0, A)
         it(1, 0, 0, 1, A)
-        it(1, 1, 0, 1, V)
+        feat(0, 0, 0)
+        load_dy(0, 1, 1)
+        feat(1, 0, 0)
+        it(1, 0, 1, 1, A)
+        qt(1, 0, 0)
+        xq(1)
+        qf(0, 0, 0)
+        ps(1, 0, 1, V)
+        qf(1, 0, 0)
+        it(1, 1, 1, 0, V)
+        it(1, 0, 1, 0, A)
+        qt(1, 0, 1)
+        load_w(0)
+        feat(0, 1, 0)
+        it(1, 1, 1, 1, V)
+        ps(1, 1, 1, V)
         load_dy(0, 0, 1)
         load_w(2)
-        qf(1, 1, 1)
-        qf(1, 0, 0)
-        load_w(1)
-        qt(1, 0, 0)
-        it(1, 1, 0, 0, A)
-        load_dy(0, 0, 0)
-        qf(1, 0, 1)
-        qt(1, 1, 0)
-        feat(0, 1, 1)
+        qt(1, 1, 1)
+        it(0, 1, 0, 1, V)
+        it(0, 0, 0, 1, V)
+        iw(0, 1, V)
+        dw(1, 3, (A, A))
+        iw(0, 0, V)
         load_dy(2, 0, 0)
-        feat(1, 1, 0)
-        iw(2, 2, V)
+        qf(0, 1, 0)
+        it(0, 0, 0, 0, V)
         load_w(3)
-        dw(1, 4, (V, A))
-        load_dy(0, 1, 0)
-        iw(2, 0, V)
-        dw(1, 5, (A, A))
-        it(0, 1, 1, 1, A)
-        it(0, 0, 1, 1, V)
-        iw(2, 1, A)
-        dw(1, 3, (A, V))
-        dw(1, 0, (A, A))
-        it(0, 1, 1, 0, V)
-        it(0, 0, 1, 0, A)
-        qf(1, 1, 0)
-        iw(1, 2, V)
-        qw(2)
-        load_w(0)
-        feat(0, 0, 0)
-        qt(0, 1, 1)
-        dw(1, 7, (A, V))
-        iw(1, 1, V)
-        load_dy(2, 0, 1)
-        iw(3, 2, V)
+        feat(0, 1, 1)
+        dw(1, 1, (A, A))
+        it(0, 1, 0, 0, A)
+        dw(1, 6, (A, A))
+        qt(0, 1, 0)
+        iw(2, 2, V)
         qf(0, 1, 1)
-        ps(2, 0, 0, V)
+        feat(1, 0, 1)
         feat(0, 0, 1)
-        iw(1, 0, V)
-        dw(1, 2, (V, A))
-        iw(3, 1, A)
-        load_w(4)
-        qt(0, 0, 1)
-        dw(1, 6, (V, A))
-        iw(3, 0, V)
-        dw(1, 1, (A, V))
-        qf(0, 0, 1)
-        load_w(5)
-        load_dy(2, 1, 1)
-        qw(1)
-        qw(3)
-        feat(2, 0, 0)
-        load_dy(2, 1, 0)
         iw(0, 2, V)
-        iw(0, 0, A)
-        qf(0, 0, 0)
-        ps(2, 0, 1, V)
-        dw(0, 7, (A, A))
-        iw(0, 1, A)
+        qt(0, 0, 0)
+        load_dy(2, 0, 1)
+        dw(1, 4, (A, A))
+        feat(1, 1, 1)
+        iw(2, 1, V)
+        iw(2, 0, A)
         qw(0)
-        iw(4, 1, V)
-        dw(0, 4, (A, A))
-        feat(0, 1, 0)
-        dw(0, 5, (A, A))
-        dw(0, 6, (A, A))
-        iw(4, 0, V)
-        iw(4, 2, V)
+        ps(2, 0, 0, V)
+        load_w(1)
+        dw(1, 5, (A, A))
+        dw(1, 7, (A, A))
+        iw(3, 2, V)
+        load_w(4)
+        iw(3, 0, V)
+        iw(3, 1, A)
+        qf(1, 0, 1)
+        load_w(5)
+        dw(0, 1, (A, A))
+        ps(2, 0, 1, V)
+        qw(2)
+        load_dy(2, 1, 1)
+        qw(3)
+        dw(0, 0, (A, A))
+        iw(1, 2, V)
+        feat(2, 0, 0)
+        iw(1, 1, V)
+        iw(1, 0, A)
+        dw(0, 2, (A, A))
+        qf(0, 0, 1)
+        load_dy(2, 1, 0)
+        qw(1)
+        qf(1, 1, 1)
         qf(2, 0, 0)
-        qw(4)
+        iw(4, 2, V)
         feat(2, 0, 1)
-        dxm(0, 1, 0)
+        dw(1, 0, (A, A))
+        iw(4, 1, V)
+        iw(4, 0, A)
+        iw(5, 2, V)
         iw(5, 0, A)
+        qw(4)
+        dw(0, 3, (A, A))
         iw(5, 1, V)
+        it(2, 1, 1, 0, A)
+        dw(1, 2, (A, V))
+        qw(5)
+        dxt(0, 0, 0)
+        dxm(0, 1, 0)
+        dxm(0, 0, 0)
+        qf(2, 0, 1)
+        it(2, 1, 1, 1, A)
+        it(2, 0, 1, 1, V)
+        it(0, 0, 1, 1, V)
         dxt(0, 1, 0)
         dxm(0, 3, 0)
-        it(2, 0, 0, 1, A)
-        iw(5, 2, V)
-        qf(2, 0, 1)
-        qw(5)
-        it(2, 1, 0, 1, A)
-        it(2, 1, 0, 0, V)
+        ps(2, 1, 1, A)
         dxm(0, 2, 0)
-        ps(2, 1, 1, V)
-        dxt(0, 0, 0)
-        it(2, 0, 0, 0, A)
-        dxm(0, 0, 0)
-        dxt(0, 1, 1)
-        qf(0, 1, 0)
-        dxt(0, 0, 1)
-        qt(2, 1, 0)
         dxm(0, 2, 1)
-        dxm(0, 1, 1)
-        dxm(0, 3, 1)
+        qt(2, 1, 1)
+        dxt(0, 1, 1)
+        dxt(0, 0, 1)
+        it(2, 0, 1, 0, V)
         ps(2, 1, 0, A)
+        dxm(0, 1, 1)
+        qt(2, 0, 1)
         dxm(0, 0, 1)
-        qt(2, 0, 0)
+        dxm(0, 3, 1)
         back(0)
+        d2(0, 1)
+        d2(0, 3)
         feat(2, 1, 1)
         feat(2, 1, 0)
-        it(0, 1, 0, 1, V)
-        d2(0, 1)
-        d2(0, 2)
-        qf(2, 1, 1)
-        dw(2, 0, (A, A))
-        d2(0, 0)
-        dxt(1, 0, 0)
-        it(2, 0, 1, 0, V)
-        qf(2, 1, 0)
-        it(0, 1, 0, 0, A)
-        d3(0, 1)
-        d3(0, 0)
-        dw(2, 1, (A, A))
-        it(0, 0, 0, 0, A)
-        qt(0, 1, 0)
-        d3(0, 2)
-        it(0, 0, 0, 1, A)
-        dxm(1, 2, 0)
-        d2(0, 3)
-        dxt(1, 1, 0)
-        dxt(1, 0, 1)
-        dxm(1, 2, 1)
-        qt(0, 0, 0)
-        dxt(1, 1, 1)
-        d3(0, 3)
-        dxm(1, 0, 0)
-        dxm(1, 0, 1)
-        it(2, 0, 1, 1, A)
-        back(1)
-        dw(2, 2, (A, A))
-        d2(1, 2)
-        dw(0, 0, (A, A))
-        dxm(1, 1, 0)
-        it(2, 1, 1, 0, A)
-        it(2, 1, 1, 1, A)
-        d2(1, 0)
-        d3(1, 2)
-        dxm(1, 1, 1)
-        qt(2, 0, 1)
-        d2(1, 1)
-        dw(0, 3, (A, A))
-        dw(0, 2, (A, A))
-        qt(2, 1, 1)
-        d3(1, 1)
-        dxm(1, 3, 0)
-        d3(1, 0)
-        dxm(1, 3, 1)
-        dw(2, 5, (A, A))
         dw(2, 4, (A, A))
+        it(0, 1, 1, 1, A)
+        it(0, 0, 1, 0, V)
+        dxt(1, 1, 0)
+        d3(0, 1)
+        qf(2, 1, 0)
+        it(2, 0, 0, 0, A)
+        qf(2, 1, 1)
+        dxm(1, 2, 0)
+        d3(0, 3)
+        d2(0, 2)
+        qt(0, 0, 1)
+        dxt(1, 0, 0)
+        dxt(1, 0, 1)
+        dxt(1, 1, 1)
+        it(0, 1, 1, 0, A)
+        d2(0, 0)
+        d3(0, 2)
+        dxm(1, 3, 0)
+        d3(0, 0)
+        qt(0, 1, 1)
+        dxm(1, 3, 1)
+        dxm(1, 2, 1)
+        it(2, 1, 0, 1, A)
+        dxm(1, 0, 0)
+        back(1)
+        dxm(1, 0, 1)
+        dw(2, 7, (A, A))
+        d2(1, 2)
         d2(1, 3)
+        dw(0, 6, (A, A))
+        d3(1, 2)
+        dw(0, 4, (A, A))
         d3(1, 3)
-        dw(2, 7, (V, V))
-        dw(2, 6, (A, V))
-        dw(2, 3, (V, V))
-        dw(0, 1, (V, A))
+        it(2, 0, 0, 1, A)
+        d2(1, 0)
+        d3(1, 0)
+        qt(2, 0, 0)
+        dw(2, 6, (A, A))
+        it(2, 1, 0, 0, A)
+        dxm(1, 1, 0)
+        dxm(1, 1, 1)
+        dw(0, 7, (A, A))
+        qt(2, 1, 0)
+        dw(0, 5, (A, A))
+        d2(1, 1)
+        dw(2, 0, (A, A))
+        d3(1, 1)
+        dw(2, 3, (A, V))
+        dw(2, 1, (A, A))
+        dw(2, 5, (V, A))
+        dw(2, 2, (V, A))

from contextlib import ExitStack

import concourse.mybir as mybir
from concourse.masks import make_identity

F32 = mybir.dt.float32
BF16 = mybir.dt.bfloat16
U32 = mybir.dt.uint32
U8 = mybir.dt.uint8
E4 = mybir.dt.float8_e4m3fn_x4
E5 = mybir.dt.float8_e5m2_x4
MULT = mybir.AluOpType.mult
ADD = mybir.AluOpType.add
COPY = mybir.ActivationFunctionType.Copy

B, S, D, H, DK = 2, 512, 768, 8, 128
E = H * DK
T = B * S
P = 128
J = 4
SORTED = ((1, 0), (1, 1), (2, 0), (2, 1))
FLOPS = 2 * 2 * T * 3 * E * D


def tile_transformerblock_pa_v_kernel(
    tc, x, g1, wq, wk, wv, r, grad_0, grad_1, grad_2, out_0, out_1, out_2, out_3
):
    nc = tc.nc
    V, A = nc.vector, nc.scalar
    grads = (grad_0, grad_1, grad_2)
    weights = (wq, wk, wv)
    w_outs = (out_1, out_2, out_3)

    with ExitStack() as ctx:
        keep = ctx.enter_context(tc.tile_pool(name="keep", bufs=1))
        rot = ctx.enter_context(tc.tile_pool(name="rot", bufs=2))
        psum = ctx.enter_context(tc.psum_pool(name="psum", bufs=8))
        ctx.enter_context(tc.manual_schedule())

        ident = keep.tile([P, P], F32, name="ident")
        ones = keep.tile([P, P], BF16, name="ones")
        g_row = keep.tile([P, D], BF16, name="g_row")
        g_bc = keep.tile([P, D], F32, name="g_bc")
        g_col = keep.tile([P, 2], F32, name="g_col")
        r_sb = keep.tile([P, B, J], F32, name="r_sb")
        nr2 = keep.tile([P, B, J], F32, name="nr2")
        c_sb = keep.tile([P, B, J], F32, name="c_sb")
        x_sb = keep.tile([P, B, J, D], BF16, name="x_sb")
        dyf_c = keep.tile([P, 6, T], U32, name="dyf_c", align_bytes=64)
        dyf_s = keep.tile([P, 6, T], U8, name="dyf_s", align_bytes=64)
        w_c = keep.tile([P, 6, D], U32, name="w_c", align_bytes=64)
        w_s = keep.tile([P, 6, D], U8, name="w_s", align_bytes=64)
        xn_c = keep.tile([P, B, D], U32, name="xn_c", align_bytes=64)
        xn_s = keep.tile([P, B, D], U8, name="xn_s", align_bytes=64)

        tiles = {}

        def get(pool, shape, dtype, tag, key, bufs, align=None):
            if (tag, key) not in tiles:
                if align:
                    t = pool.tile(shape, dtype, name=tag, bufs=bufs, align_bytes=align)
                else:
                    t = pool.tile(shape, dtype, name=tag, bufs=bufs)
                tiles[tag, key] = t
            return tiles[tag, key]

        def load_x(b):
            src = x[b].rearrange("(p j) d -> p j d", j=J)
            step = 256 if b == 0 else D
            for lo in range(0, D, step):
                nc.sync.dma_start(out=x_sb[:, b, :, lo : lo + step], in_=src[:, :, lo : lo + step])

        def dy_raw(a, b, g):
            shape = [P, 4, J, DK] if (a, b) in SORTED else [P, J, 512]
            return get(rot, shape, BF16, "dy_raw", (a, b, g), 8)

        def load_dy(a, b, g):
            t = dy_raw(a, b, g)
            src = grads[a][b][4 * g : 4 * g + 4]
            if (a, b) not in SORTED:
                src = src.rearrange("h (p j) d -> p j h d", j=J)
                for j in range(J):
                    nc.sync.dma_start(
                        out=t[:, j, :].rearrange("p (h d) -> p h d", d=DK), in_=src[:, j]
                    )
            else:
                nc.sync.dma_start(
                    out=t[:].rearrange("p h j d -> p h (j d)"),
                    in_=src.rearrange("h (p j) d -> p h (j d)", j=J),
                )

        def copy(eng, out, in_):
            if eng is A:
                nc.scalar.copy(out=out, in_=in_)
            else:
                nc.vector.tensor_copy(out=out, in_=in_)

        def ps(a, b, g, eng):
            t = get(rot, [P, J, 2, P], F32, "srt", (a, b, g), 2)
            words = dy_raw(a, b, g)[:].rearrange("p h j d -> p (h j d)").bitcast(F32)
            words = words.rearrange("p (h j w) -> p j h w", h=4, j=J)
            for u in range(2):
                copy(eng, t[:, :, u, :].rearrange("p j (h q) -> p j h q", h=4), words[:, :, :, u::2])

        def w_raw(n):
            return get(rot, [P, J, D], BF16, "w_raw", n, 3)

        def load_w(n):
            a, half = divmod(n, 2)
            src = weights[a][512 * half : 512 * half + 512, :]
            nc.sync.dma_start(out=w_raw(n)[:], in_=src.rearrange("(p j) d -> p j d", j=J))

        def grouped_d(key):
            return get(rot, [P, D, J], BF16, "gw", key, 2, 64)

        def norm(b, k):
            lo, hi = 256 * k, 256 * k + 256
            t = get(rot, [P, J, D], F32, "big", ("x", b), 2)
            for j in range(J):
                xs, rs = x_sb[:, b, j, lo:hi], r_sb[:, b, j : j + 1]
                nc.scalar.activation(out=t[:, j, lo:hi], in_=xs, func=COPY, scale=rs)
            nc.vector.tensor_tensor(
                out=grouped_d(("x", b))[:, lo:hi, :],
                in0=t[:, :, lo:hi].rearrange("p j d -> p d j"),
                in1=gps[k // 2][:, lo % 512 : lo % 512 + 256].unsqueeze(2).to_broadcast([P, 256, J]),
                op=MULT,
            )

        def quant_d(codes, scales, src):
            flat = src[:].rearrange("p d j -> p (d j)")
            for lo, hi in ((0, 512), (512, 768)):
                nc.vector.quantize_mx(
                    out=codes[:, lo:hi].bitcast(E4), scales=scales[:, lo:hi], in_=flat[:, 4 * lo : 4 * hi]
                )

        def xq(b):
            quant_d(xn_c[:, b, :], xn_s[:, b, :], grouped_d(("x", b)))

        def feat(a, b, g):
            if (a, b) not in SORTED:
                words = dy_raw(a, b, g)[:].rearrange("p j f -> p (j f)").bitcast(F32)
                words = words.rearrange("p (j w u) -> p j u w", j=J, u=2)
            else:
                words = tiles["srt", (a, b, g)]
            t = get(rot, [P, 2048], BF16, "gf", (a, b, g), 3, 64)
            out_words = t[:].bitcast(F32)
            for jj in range(2):
                bank = psum.tile([P, 2, 2, P], F32, name="bank")
                for j2 in range(2):
                    for u in range(2):
                        nc.tensor.transpose(bank[:, j2, u, :], words[:, 2 * jj + j2, u, :], ident[:])
                nc.scalar.copy(
                    out=out_words[:, 512 * jj : 512 * jj + 512].rearrange("p (j q u) -> p j q u", j=2, u=2),
                    in_=bank[:].rearrange("p j u q -> p j q u"),
                )

        def qf(a, b, g):
            n = 2 * a + g
            nc.vector.quantize_mx(
                out=dyf_c[:, n, S * b : S * b + S].bitcast(E5),
                scales=dyf_s[:, n, S * b : S * b + S],
                in_=tiles["gf", (a, b, g)][:],
            )

        def interleave(eng, out, in_):
            o = out.rearrange("p (c i) j -> p c j i", i=4)
            n = in_.rearrange("p j (c i) -> p c j i", i=4)
            copy(eng, o, n)

        def it(a, b, g, k, eng):
            t = get(rot, [P, 512, J], BF16, "gt", (a, b, g), 3, 64)
            o = t[:, 256 * k : 256 * k + 256, :]
            raw = dy_raw(a, b, g)
            if (a, b) not in SORTED:
                interleave(eng, o, raw[:, :, 256 * k : 256 * k + 256])
            else:
                copy(
                    eng,
                    o.rearrange("p (h c i) j -> p h c j i", h=2, i=4),
                    raw[:, 2 * k : 2 * k + 2].rearrange("p h j (c i) -> p h c j i", i=4),
                )

        def dyt(a):
            return (
                get(rot, [P, B, E], U32, "dyt_c", a, 2, 64),
                get(rot, [P, B, E], U8, "dyt_s", a, 2, 64),
            )

        def qt(a, b, g):
            codes, scales = dyt(a)
            nc.vector.quantize_mx(
                out=codes[:, b, 512 * g : 512 * g + 512].bitcast(E5),
                scales=scales[:, b, 512 * g : 512 * g + 512],
                in_=tiles["gt", (a, b, g)][:].rearrange("p f j -> p (f j)"),
            )

        def iw(n, k, eng):
            lo, hi = 256 * k, 256 * k + 256
            interleave(eng, grouped_d(n)[:, lo:hi, :], w_raw(n)[:, :, lo:hi])

        def qw(n):
            quant_d(w_c[:, n, :], w_s[:, n, :], grouped_d(n))

        def dw(a, h, engines):
            codes, scales = dyt(a)
            t = rot.tile([P, D], F32, name="res", bufs=4)
            for lo, cut, eng in ((0, 0, engines[0]), (256, 256, engines[1])):
                bank = psum.tile([P, 512], F32, name="bank")
                for b in range(B):
                    nc.tensor.matmul_mx(
                        out=bank[:],
                        lhsT=codes[:, b, P * h : P * h + P].bitcast(E5),
                        lhsT_scale=scales[:, b, P * h : P * h + P],
                        rhs=xn_c[:, b, lo : lo + 512].bitcast(E4),
                        rhs_scale=xn_s[:, b, lo : lo + 512],
                        start=(b == 0),
                        stop=(b == B - 1),
                    )
                copy(eng, t[:, lo + cut : lo + 512], bank[:, cut:512])
            nc.sync.dma_start(out=w_outs[a][P * h : P * h + P, :], in_=t[:])

        def dxt(b, i, part):
            pt = get(psum, [P, 512], F32, "bank", ("t", b, i), None)
            d0 = 512 + P * i
            for n in (range(4), range(4, 6))[part]:
                nc.tensor.matmul_mx(
                    out=pt[:],
                    lhsT=w_c[:, n, d0 : d0 + P].bitcast(E4),
                    lhsT_scale=w_s[:, n, d0 : d0 + P],
                    rhs=dyf_c[:, n, S * b : S * b + S].bitcast(E5),
                    rhs_scale=dyf_s[:, n, S * b : S * b + S],
                    start=(n == 0),
                    stop=(n == 5),
                )
            if part == 1:
                t = get(rot, [P, 2, 512], F32, "hT", b, 1)
                nc.scalar.activation(out=t[:, i, :], in_=pt[:], func=COPY, scale=g_col[:, i : i + 1])

        def hr(b):
            return get(rot, [P, J, D], F32, "big", ("h", b), 2)

        def back(b):
            for jj in range(2):
                bank = psum.tile([P, 2, 2, P], F32, name="bank")
                for j2 in range(2):
                    for i in range(2):
                        j = 2 * jj + j2
                        nc.tensor.transpose(
                            bank[:, j2, i, :], tiles["hT", b][:, i, P * j : P * j + P], ident[:]
                        )
                for j2 in range(2):
                    j = 2 * jj + j2
                    nc.scalar.activation(
                        out=hr(b)[:, j, 512:768],
                        in_=bank[:, j2].rearrange("p i q -> p (i q)"),
                        func=COPY,
                        scale=r_sb[:, b, j : j + 1],
                    )

        def dxm(b, j, part):
            pt = get(psum, [P, 512], F32, "bank", ("m", b, j), None)
            t0 = S * b + P * j
            for n in (range(4), range(4, 6))[part]:
                nc.tensor.matmul_mx(
                    out=pt[:],
                    lhsT=dyf_c[:, n, t0 : t0 + P].bitcast(E5),
                    lhsT_scale=dyf_s[:, n, t0 : t0 + P],
                    rhs=w_c[:, n, 0:512].bitcast(E4),
                    rhs_scale=w_s[:, n, 0:512],
                    start=(n == 0),
                    stop=(n == 5),
                )
            if part == 1:
                nc.vector.scalar_tensor_tensor(
                    out=hr(b)[:, j, 0:512],
                    in0=pt[:],
                    scalar=r_sb[:, b, j : j + 1],
                    in1=g_bc[:, 0:512],
                    op0=MULT,
                    op1=MULT,
                )

        def d2(b, j):
            junk = rot.tile([P, D], F32, name="junk", bufs=1)
            nc.vector.scalar_tensor_tensor(
                out=junk[:],
                in0=hr(b)[:, j, :],
                scalar=nr2[:, b, j : j + 1],
                in1=x_sb[:, b, j, :],
                op0=MULT,
                op1=MULT,
                accum_out=c_sb[:, b, j : j + 1],
            )

        def d3(b, j):
            nc.vector.scalar_tensor_tensor(
                out=hr(b)[:, j, :],
                in0=x_sb[:, b, j, :],
                scalar=c_sb[:, b, j : j + 1],
                in1=hr(b)[:, j, :],
                op0=MULT,
                op1=ADD,
            )
            dst = out_0[b].rearrange("(p j) d -> p j d", j=J)
            nc.sync.dma_start(out=dst[:, j], in_=hr(b)[:, j, :])

        nc.gpsimd.memset(g_row[:], 0.0)
        nc.gpsimd.memset(ones[:], 1.0)
        make_identity(nc, ident[:])
        nc.sync.dma_start(out=g_row[0:1, :], in_=g1.rearrange("(o d) -> o d", o=1))
        nc.sync.dma_start(out=r_sb[:], in_=r.rearrange("b (p j) -> p b j", j=J))
        dummy = keep.tile([P, 1], F32, name="dummy")
        nc.vector.memset(dummy[:], 0.0)
        nc.scalar.activation(out=dummy[:], in_=dummy[:], func=COPY)
        gp0 = psum.tile([P, 512], F32, name="bank")
        gp1 = psum.tile([P, 512], F32, name="bank")
        gps = (gp0, gp1)
        nc.tensor.matmul(gp0[:], lhsT=ones[:], rhs=g_row[:, 0:512], start=True, stop=True)
        nc.tensor.matmul(gp1[:, 0:256], lhsT=ones[:], rhs=g_row[:, 512:768], start=True, stop=True)
        nc.vector.tensor_copy(out=g_bc[:, 0:512], in_=gp0[:])
        nc.vector.tensor_copy(out=g_bc[:, 512:768], in_=gp1[:, 0:256])
        gp2 = psum.tile([P, 2, 2, P], F32, name="bank")
        for i in range(2):
            nc.tensor.transpose(gp2[:, 0, i, :], g_bc[:, 512 + P * i : 640 + P * i], ident[:])
        nc.vector.scalar_tensor_tensor(
            out=nr2[:], in0=r_sb[:], scalar=-1.0 / D, in1=r_sb[:], op0=MULT, op1=MULT
        )
        nc.vector.tensor_copy(out=g_col[:], in_=gp2[:, 0, :, 0])
        load_x(0)
        norm(0, 0)
        load_dy(1, 1, 0)
        load_dy(1, 0, 0)
        load_x(1)
        load_dy(0, 0, 0)
        norm(0, 1)
        it(1, 1, 0, 1, V)
        norm(0, 2)
        ps(1, 1, 0, A)
        it(1, 0, 0, 0, V)
        xq(0)
        load_dy(0, 1, 0)
        load_dy(1, 0, 1)
        ps(1, 0, 0, V)
        load_dy(1, 1, 1)
        it(1, 1, 0, 0, A)
        qt(1, 1, 0)
        feat(1, 1, 0)
        qf(1, 1, 0)
        norm(1, 2)
        norm(1, 1)
        norm(1, 0)
        it(1, 0, 0, 1, A)
        feat(0, 0, 0)
        load_dy(0, 1, 1)
        feat(1, 0, 0)
        it(1, 0, 1, 1, A)
        qt(1, 0, 0)
        xq(1)
        qf(0, 0, 0)
        ps(1, 0, 1, V)
        qf(1, 0, 0)
        it(1, 1, 1, 0, V)
        it(1, 0, 1, 0, A)
        qt(1, 0, 1)
        load_w(0)
        feat(0, 1, 0)
        it(1, 1, 1, 1, V)
        ps(1, 1, 1, V)
        load_dy(0, 0, 1)
        load_w(2)
        qt(1, 1, 1)
        it(0, 1, 0, 1, V)
        it(0, 0, 0, 1, V)
        iw(0, 1, V)
        dw(1, 3, (A, A))
        iw(0, 0, V)
        load_dy(2, 0, 0)
        qf(0, 1, 0)
        it(0, 0, 0, 0, V)
        load_w(3)
        feat(0, 1, 1)
        dw(1, 1, (A, A))
        it(0, 1, 0, 0, A)
        dw(1, 6, (A, A))
        qt(0, 1, 0)
        iw(2, 2, V)
        qf(0, 1, 1)
        feat(1, 0, 1)
        feat(0, 0, 1)
        iw(0, 2, V)
        qt(0, 0, 0)
        load_dy(2, 0, 1)
        dw(1, 4, (A, A))
        feat(1, 1, 1)
        iw(2, 1, V)
        iw(2, 0, A)
        qw(0)
        ps(2, 0, 0, V)
        load_w(1)
        dw(1, 5, (A, A))
        dw(1, 7, (A, A))
        iw(3, 2, V)
        load_w(4)
        iw(3, 0, V)
        iw(3, 1, A)
        qf(1, 0, 1)
        load_w(5)
        dw(0, 1, (A, A))
        ps(2, 0, 1, V)
        qw(2)
        load_dy(2, 1, 1)
        qw(3)
        dw(0, 0, (A, A))
        iw(1, 2, V)
        feat(2, 0, 0)
        iw(1, 1, V)
        iw(1, 0, A)
        dw(0, 2, (A, A))
        qf(0, 0, 1)
        load_dy(2, 1, 0)
        qw(1)
        qf(1, 1, 1)
        qf(2, 0, 0)
        iw(4, 2, V)
        feat(2, 0, 1)
        dw(1, 0, (A, A))
        iw(4, 1, V)
        iw(4, 0, A)
        iw(5, 2, V)
        iw(5, 0, A)
        qw(4)
        dw(0, 3, (A, A))
        iw(5, 1, V)
        it(2, 1, 1, 0, A)
        dw(1, 2, (A, V))
        qw(5)
        dxt(0, 0, 0)
        dxm(0, 1, 0)
        dxm(0, 0, 0)
        qf(2, 0, 1)
        it(2, 1, 1, 1, A)
        it(2, 0, 1, 1, V)
        it(0, 0, 1, 1, V)
        dxt(0, 1, 0)
        dxm(0, 3, 0)
        ps(2, 1, 1, A)
        dxm(0, 2, 0)
        dxm(0, 2, 1)
        qt(2, 1, 1)
        dxt(0, 1, 1)
        dxt(0, 0, 1)
        it(2, 0, 1, 0, V)
        ps(2, 1, 0, A)
        dxm(0, 1, 1)
        qt(2, 0, 1)
        dxm(0, 0, 1)
        dxm(0, 3, 1)
        back(0)
        d2(0, 1)
        d2(0, 3)
        feat(2, 1, 1)
        feat(2, 1, 0)
        dw(2, 4, (A, A))
        it(0, 1, 1, 1, A)
        it(0, 0, 1, 0, V)
        dxt(1, 1, 0)
        d3(0, 1)
        qf(2, 1, 0)
        it(2, 0, 0, 0, A)
        qf(2, 1, 1)
        dxm(1, 2, 0)
        d3(0, 3)
        d2(0, 2)
        qt(0, 0, 1)
        dxt(1, 0, 0)
        dxt(1, 0, 1)
        dxt(1, 1, 1)
        it(0, 1, 1, 0, A)
        d2(0, 0)
        d3(0, 2)
        dxm(1, 3, 0)
        d3(0, 0)
        qt(0, 1, 1)
        dxm(1, 3, 1)
        dxm(1, 2, 1)
        it(2, 1, 0, 1, A)
        dxm(1, 0, 0)
        back(1)
        dxm(1, 0, 1)
        dw(2, 7, (A, A))
        d2(1, 2)
        d2(1, 3)
        dw(0, 6, (A, A))
        d3(1, 2)
        dw(0, 4, (A, A))
        d3(1, 3)
        it(2, 0, 0, 1, A)
        d2(1, 0)
        d3(1, 0)
        qt(2, 0, 0)
        dw(2, 6, (A, A))
        it(2, 1, 0, 0, A)
        dxm(1, 1, 0)
        dxm(1, 1, 1)
        dw(0, 7, (A, A))
        qt(2, 1, 0)
        dw(0, 5, (A, A))
        d2(1, 1)
        dw(2, 0, (A, A))
        d3(1, 1)
        dw(2, 3, (A, V))
        dw(2, 1, (A, A))
        dw(2, 5, (V, A))
        dw(2, 2, (V, A))
